import numpy as np
import ml_dtypes


def mxq(x, axis, fmt="e4m3"):
    dtype, down = {"e4m3": (ml_dtypes.float8_e4m3fn, 7), "e5m2": (ml_dtypes.float8_e5m2, 14)}[fmt]
    v = np.moveaxis(np.asarray(x, np.float32).astype(ml_dtypes.bfloat16).astype(np.float64), axis, -1)
    blocks = v.reshape(v.shape[:-1] + (-1, 32))
    amax = np.abs(blocks).max(-1, keepdims=True)
    byte = np.maximum(np.where(amax > 0, np.frexp(amax)[1] - 1 + 127, 0) - down, 1)
    scale = np.exp2(byte - 127.0)
    codes = (blocks / scale).astype(np.float32).astype(dtype).astype(np.float64)
    return np.moveaxis((codes * scale).reshape(v.shape), -1, axis)


WIDE = False


def mx_kscale(k):
    if not WIDE:
        return np.ones(k)
    levels = np.array([10, -10, 5, -5, 0])
    a = np.random.permutation(np.resize(levels, k // 512 * 4)).reshape(k // 512, 4)
    idx = np.arange(k)
    return np.exp2(a[idx // 512, idx % 128 // 32])


BF16 = ml_dtypes.bfloat16


def bf(x):
    return np.asarray(x, np.float32).astype(BF16)


def f64(x):
    return np.asarray(x).astype(np.float64)


E2M1 = np.array([0.0, 0.5, 1.0, 1.5, 2.0, 3.0, 4.0, 6.0, -0.0, -0.5, -1.0, -1.5, -2.0, -3.0, -4.0, -6.0])


def pack_weight(w, fmt):
    k, n = w.shape
    w = f64(bf(w)).reshape(k // 32, 32, n)
    amax = np.abs(w).max(1)
    if fmt == "e4m3":
        byte = np.frexp(amax)[1] - 1 + 127 - 7
    else:
        mant, ex = np.frexp(amax / 6.0)
        byte = np.where(mant > 0.5, ex, ex - 1) + 127
    byte = np.clip(np.where(amax > 0, byte, 1), 1, 254)
    scaled = (w * np.exp2(127.0 - byte)[:, None, :]).reshape(k, n).astype(np.float32)
    by_word = np.ascontiguousarray(scaled.reshape(k // 512, 128, 4, n).transpose(0, 1, 3, 2))
    if fmt == "e4m3":
        words = by_word.astype(ml_dtypes.float8_e4m3fn).view(np.uint8)
    else:
        c = by_word.astype(ml_dtypes.float4_e2m1fn).view(np.uint8) & 0xF
        words = c[..., 0::2] | (c[..., 1::2] << 4)
    return np.ascontiguousarray(words), np.ascontiguousarray(byte.astype(np.uint8).reshape(k // 512, 16, n))


def unpack_weight(words, scales, fmt):
    g, p, n, _ = words.shape
    if fmt == "e4m3":
        vals = np.ascontiguousarray(words).view(ml_dtypes.float8_e4m3fn).astype(np.float64)
    else:
        nib = np.empty((g, p, n, 4), np.uint8)
        nib[..., 0::2] = words & 0xF
        nib[..., 1::2] = words >> 4
        vals = E2M1[nib]
    vals = vals * np.repeat(np.exp2(scales.astype(np.float64) - 127.0), 8, axis=1)[..., None]
    return vals.transpose(0, 1, 3, 2).reshape(g * 512, n)


B, I, H = 128, 1024, 2048
K = I + H
FMT = "e4m3"


def setup_inputs():
    s = mx_kscale(I)
    sk = np.concatenate([s, np.ones(H)])
    x = bf(np.random.standard_normal((B, I)) * s)
    h = bf(np.random.standard_normal((B, H)))
    time_delta = bf(np.random.uniform(0.0, 1.0, (B, 1)))
    W_mod_words, W_mod_scales = pack_weight(np.random.standard_normal((K, H)) * 0.6 / np.sqrt(K) / sk[:, None], FMT)
    b_mod = bf(np.random.standard_normal(H) * 0.2)
    W_tgt_words, W_tgt_scales = pack_weight(np.random.standard_normal((K, H)) * 0.6 / np.sqrt(K) / sk[:, None], FMT)
    b_tgt = bf(np.random.standard_normal(H) * 0.2)
    log_tau = bf(np.random.standard_normal(H) * 0.2)
    bias = bf(np.random.standard_normal(H) * 0.1)
    return {"x": x,
            "h": h,
            "time_delta": time_delta,
            "W_mod_words": W_mod_words,
            "W_mod_scales": W_mod_scales,
            "b_mod": b_mod,
            "W_tgt_words": W_tgt_words,
            "W_tgt_scales": W_tgt_scales,
            "b_tgt": b_tgt,
            "log_tau": log_tau,
            "bias": bias}


def reference(x, h, time_delta, W_mod_words, W_mod_scales, b_mod, W_tgt_words, W_tgt_scales, b_tgt, log_tau, bias):
    hf = f64(h)
    combined = np.concatenate([f64(x), hf], axis=-1)
    cq = mxq(combined, 1, "e4m3")
    f = np.tanh((cq @ unpack_weight(W_mod_words, W_mod_scales, FMT)) + f64(b_mod))
    a = np.tanh((cq @ unpack_weight(W_tgt_words, W_tgt_scales, FMT)) + f64(b_tgt))
    tau = np.exp(f64(log_tau))[None, :]
    tau_sys = tau / (1.0 + tau * np.abs(f))
    decay = np.exp(-f64(time_delta) / (tau_sys + 1e-6))
    h_new = decay * hf + (1.0 - decay) * (a + f64(bias))
    return h_new

@@ -1,0 +1,298 @@
+from contextlib import ExitStack
+
+import concourse.masks as masks
+import concourse.mybir as mybir
+
+F32 = mybir.dt.float32
+BF16 = mybir.dt.bfloat16
+I32 = mybir.dt.int32
+U32 = mybir.dt.uint32
+U8 = mybir.dt.uint8
+FP8X4 = mybir.dt.float8_e4m3fn_x4
+ALU = mybir.AluOpType
+ACT = mybir.ActivationFunctionType
+
+P = 128
+I_DIM = 1024
+H_DIM = 2048
+K_DIM = I_DIM + H_DIM
+GROUPS = K_DIM // 512
+CHUNK = 512
+EPS = 1e-6
+
+FLOPS = 2 * P * K_DIM * 2 * H_DIM
+
+
+def tile_ltccell_w_kernel(
+    tc,
+    x,
+    h,
+    time_delta,
+    W_mod_words,
+    W_mod_scales,
+    b_mod,
+    W_tgt_words,
+    W_tgt_scales,
+    b_tgt,
+    log_tau,
+    bias,
+    out,
+):
+    nc = tc.nc
+    with ExitStack() as ctx:
+        keep = ctx.enter_context(tc.tile_pool(name="keep", bufs=1))
+        work = ctx.enter_context(tc.tile_pool(name="work", bufs=3))
+        psum = ctx.enter_context(tc.psum_pool(name="psum", bufs=8))
+        ctx.enter_context(tc.manual_schedule())
+
+        words_mod = keep.tile([P, GROUPS, H_DIM], I32, align_bytes=64)
+        words_tgt = keep.tile([P, GROUPS, H_DIM], I32, align_bytes=64)
+        planes = keep.tile([P, 3, H_DIM], U8, align_bytes=64)
+        c_sb = keep.tile([P, K_DIM], BF16, align_bytes=64)
+        grouped = keep.tile([P, GROUPS * 512], BF16, align_bytes=64)
+        c_codes = keep.tile([P, GROUPS * P], U32, align_bytes=64)
+        c_scales = keep.tile([P, GROUPS * P], U8, align_bytes=64)
+        rows = keep.tile([P, H_DIM], BF16)
+        ltr = keep.tile([P, P], BF16)
+        ident_f = keep.tile([P, P], F32)
+        ident_b = keep.tile([P, P], BF16)
+        warm = keep.tile([P, 1], F32)
+        warm_out = keep.tile([P, 1], F32)
+        dt_sb = keep.tile([P, 1], BF16)
+        ndt = keep.tile([P, 1], F32)
+        tau = keep.tile([P, 16], F32)
+        tau_eps = keep.tile([P, 16], F32)
+        alpha = keep.tile([P, 16], F32)
+        beta = keep.tile([P, 16], F32)
+        bmod_b = keep.tile([P, H_DIM], BF16)
+        btgt_b = keep.tile([P, H_DIM], BF16)
+        alpha_b = keep.tile([P, H_DIM], F32)
+        beta_b = keep.tile([P, H_DIM], F32)
+        hb = keep.tile([P, H_DIM], F32)
+        q_all = keep.tile([P, H_DIM], F32)
+
+        words = {"mod": words_mod, "tgt": words_tgt}
+        src_words = {
+            "mod": W_mod_words.rearrange("g p n t -> p g (n t)").bitcast(I32),
+            "tgt": W_tgt_words.rearrange("g p n t -> p g (n t)").bitcast(I32),
+        }
+        h_sb = c_sb[:, I_DIM:K_DIM]
+
+        def plane_of(w, g):
+            if w == "mod":
+                return (0, 4 * g) if g < 4 else (1, 4 * (g - 4))
+            return (1, 8 + 4 * g) if g < 2 else (2, 4 * (g - 2))
+
+        nc.vector.memset(warm[:], 0.0)
+        nc.vector.memset(planes[:].bitcast(I32), 0)
+        nc.vector.memset(ltr[:].bitcast(I32), 0)
+        nc.vector.memset(rows[:].bitcast(I32), 0)
+        nc.scalar.activation(out=warm_out[:], in_=warm[:], func=ACT.Exp)
+        masks.make_identity(nc, ident_f[:])
+        masks.make_identity(nc, ident_b[:])
+
+        nc.sync.dma_start(out=c_sb[:, 0:I_DIM], in_=x)
+        nc.sync.dma_start(out=c_sb[:, I_DIM:K_DIM], in_=h)
+
+        def load_planes(slot, first_row, src):
+            n_rows = 4 * src.shape[0]
+            for q in range(4):
+                lo = 32 * q + first_row
+                nc.sync.dma_start(
+                    out=planes[lo : lo + n_rows, slot, :].bitcast(I32),
+                    in_=src[:, 4 * q : 4 * q + 4, :].bitcast(I32),
+                )
+
+        load_planes(0, 0, W_mod_scales[0:4])
+        load_planes(1, 0, W_mod_scales[4:6])
+        load_planes(1, 8, W_tgt_scales[0:2])
+        load_planes(2, 0, W_tgt_scales[2:6])
+
+        loads = [
+            ("mod", 0, 2, 0, 1024),
+            ("mod", 2, 4, 0, 1024),
+            ("mod", 4, 6, 0, 1024),
+            ("mod", 0, 2, 1024, 2048),
+            ("mod", 2, 4, 1024, 2048),
+            ("mod", 4, 6, 1024, 2048),
+            ("tgt", 0, 2, 0, 1024),
+            ("tgt", 2, 4, 0, 1024),
+            ("tgt", 4, 6, 0, 1024),
+            ("tgt", 0, 3, 1024, 1536),
+            ("tgt", 3, 6, 1024, 1536),
+            ("tgt", 0, 3, 1536, 2048),
+            ("tgt", 3, 5, 1536, 2048),
+            ("tgt", 5, 6, 1536, 2048),
+        ]
+        for w, g0, g1, n0, n1 in loads:
+            nc.sync.dma_start(out=words[w][:, g0:g1, n0:n1], in_=src_words[w][:, g0:g1, n0:n1])
+
+        nc.gpsimd.dma_start(out=ltr[0:16, :], in_=log_tau.rearrange("(c j) -> c j", c=16))
+        nc.gpsimd.dma_start(out=rows[0:1, :], in_=b_mod.unsqueeze(0))
+        with nc.allow_non_contiguous_dma(reason="one bf16 value for each partition"):
+            nc.gpsimd.dma_start(out=dt_sb[:], in_=time_delta)
+        nc.gpsimd.dma_start(out=rows[32:33, :], in_=b_tgt.unsqueeze(0))
+        nc.gpsimd.dma_start(out=rows[64:65, :], in_=bias.unsqueeze(0))
+
+        c32 = c_sb[:].bitcast(F32)
+        g32 = grouped[:].bitcast(F32).rearrange("p (g t u) -> p g t u", g=GROUPS, t=P, u=2)
+        for b in range(3):
+            xt = psum.tile([P, 2, 2, P], F32, tag="bank", name="xt%d" % b)
+            for gi in range(2):
+                g = 2 * b + gi
+                for u in range(2):
+                    nc.tensor.transpose(
+                        xt[:, gi, u, :], c32[:, 256 * g + u : 256 * (g + 1) : 2], ident_f[:]
+                    )
+            src = xt[:].rearrange("p g u t -> p g t u")
+            if b == 1:
+                nc.scalar.copy(out=g32[:, 2 * b : 2 * b + 2], in_=src)
+            else:
+                nc.vector.tensor_copy(out=g32[:, 2 * b : 2 * b + 2], in_=src)
+        nc.vector.quantize_mx(
+            out=c_codes[:, 0:256].bitcast(FP8X4), scales=c_scales[:, 0:256], in_=grouped[:, 0:1024]
+        )
+        nc.vector.quantize_mx(
+            out=c_codes[:, 256:768].bitcast(FP8X4),
+            scales=c_scales[:, 256:768],
+            in_=grouped[:, 1024:3072],
+        )
+
+        ps_lt = psum.tile([P, P], BF16, tag="bank", name="ps_lt")
+        nc.tensor.transpose(ps_lt[:], ltr[:], ident_b[:])
+        nc.scalar.activation(out=tau[:], in_=ps_lt[:, 0:16], func=ACT.Exp)
+        nc.vector.tensor_scalar(out=ndt[:], in0=dt_sb[:], scalar1=-1.0, scalar2=None, op0=ALU.mult)
+        nc.vector.tensor_scalar(out=tau_eps[:], in0=tau[:], scalar1=EPS, scalar2=None, op0=ALU.add)
+        nc.vector.reciprocal(out=alpha[:], in_=tau_eps[:])
+        nc.vector.tensor_scalar(
+            out=beta[:], in0=alpha[:], scalar1=-EPS, scalar2=1.0, op0=ALU.mult, op1=ALU.add
+        )
+
+        def spread_row(row, half, name):
+            ps = psum.tile([P, 1024], BF16, tag="bank", name=name)
+            for i in range(2):
+                n0 = 1024 * half + 512 * i
+                nc.tensor.matmul(
+                    ps[:, 512 * i : 512 * (i + 1)],
+                    lhsT=ident_b[:, row : row + 1].to_broadcast([P, P]),
+                    rhs=rows[:, n0 : n0 + 512],
+                    start=True,
+                    stop=True,
+                )
+            return ps
+
+        def spread_small(small, j, name):
+            ps = psum.tile([P, CHUNK], F32, tag="bank", name=name)
+            for i in range(4):
+                c = 4 * j + i
+                nc.tensor.transpose(
+                    ps[:, P * i : P * (i + 1)], small[:, c : c + 1].to_broadcast([P, P]), ident_f[:]
+                )
+            return ps
+
+        def prep_f(half):
+            ps = spread_row(0, half, "ps_bmod%d" % half)
+            nc.scalar.copy(out=bmod_b[:, 1024 * half : 1024 * (half + 1)], in_=ps[:])
+            for j in (2 * half, 2 * half + 1):
+                cols = slice(CHUNK * j, CHUNK * (j + 1))
+                ps_b = spread_small(beta, j, "ps_beta%d" % j)
+                nc.vector.tensor_copy(out=beta_b[:, cols], in_=ps_b[:])
+                ps_a = spread_small(alpha, j, "ps_alpha%d" % j)
+                nc.scalar.copy(out=alpha_b[:, cols], in_=ps_a[:])
+
+        def prep_a(half):
+            cols = slice(1024 * half, 1024 * (half + 1))
+            ps = spread_row(32, half, "ps_btgt%d" % half)
+            nc.scalar.copy(out=btgt_b[:, cols], in_=ps[:])
+            ps2 = spread_row(64, half, "ps_bias%d" % half)
+            nc.vector.tensor_tensor(out=hb[:, cols], in0=h_sb[:, cols], in1=ps2[:], op=ALU.subtract)
+
+        def mx_passes(w, accs, g0, g1):
+            for g in range(g0, g1):
+                slot, k = plane_of(w, g)
+                for j in sorted(accs):
+                    cols = slice(CHUNK * j, CHUNK * (j + 1))
+                    nc.tensor.matmul_mx(
+                        out=accs[j][:],
+                        lhsT=c_codes[:, P * g : P * (g + 1)].bitcast(FP8X4),
+                        lhsT_scale=c_scales[:, P * g : P * (g + 1)],
+                        rhs=words[w][:, g, cols].bitcast(FP8X4),
+                        rhs_scale=planes[k:P, slot, cols],
+                        start=(g == 0),
+                        stop=(g == GROUPS - 1),
+                    )
+
+        def open_groups(w, chunks):
+            accs = {}
+            for j in chunks:
+                acc = psum.tile([P, CHUNK], F32, tag="bank", name="z_%s%d" % (w, j))
+                accs[j] = acc
+            return accs
+
+        def f_side(accs):
+            chunks = sorted(accs)
+            t_u = {}
+            t_a1 = {}
+            t_q = {}
+            t_r = {}
+            for j in chunks:
+                cols = slice(CHUNK * j, CHUNK * (j + 1))
+                u_t = work.tile([P, CHUNK], F32, tag="u", name="u%d" % j)
+                t_u[j] = u_t
+                nc.vector.tensor_tensor(out=u_t[:], in0=accs[j][:], in1=bmod_b[:, cols], op=ALU.add)
+            for j in chunks:
+                nc.scalar.activation(out=t_u[j][:], in_=t_u[j][:], func=ACT.Abs)
+                nc.scalar.activation(out=t_u[j][:], in_=t_u[j][:], func=ACT.Tanh)
+            for j in chunks:
+                cols = slice(CHUNK * j, CHUNK * (j + 1))
+                a1_t = work.tile([P, CHUNK], F32, tag="a1", name="a1_%d" % j)
+                r_t = work.tile([P, CHUNK], F32, tag="r", name="r%d" % j)
+                t_a1[j] = a1_t
+                t_r[j] = r_t
+                nc.vector.tensor_tensor(out=a1_t[:], in0=t_u[j][:], in1=beta_b[:, cols], op=ALU.mult)
+                nc.vector.tensor_tensor(out=r_t[:], in0=a1_t[:], in1=alpha_b[:, cols], op=ALU.add)
+            for j in chunks:
+                q_t = work.tile([P, CHUNK], F32, tag="q", name="q%d" % j)
+                t_q[j] = q_t
+                nc.scalar.activation(out=q_t[:], in_=t_a1[j][:], func=ACT.Copy, bias=1.0, scale=-EPS)
+            for j in chunks:
+                nc.vector.tensor_tensor(out=t_r[j][:], in0=t_r[j][:], in1=t_q[j][:], op=ALU.mult)
+            for j in chunks:
+                cols = slice(CHUNK * j, CHUNK * (j + 1))
+                nc.scalar.activation(out=t_r[j][:], in_=t_r[j][:], func=ACT.Exp, scale=ndt[:, 0:1])
+                nc.scalar.activation(
+                    out=q_all[:, cols], in_=t_r[j][:], func=ACT.Copy, bias=1.0, scale=-1.0
+                )
+
+        def a_side(accs):
+            chunks = sorted(accs)
+            t_a = {}
+            for j in chunks:
+                cols = slice(CHUNK * j, CHUNK * (j + 1))
+                a_t = work.tile([P, CHUNK], F32, tag="a", name="a%d" % j)
+                t_a[j] = a_t
+                nc.vector.tensor_tensor(out=a_t[:], in0=accs[j][:], in1=btgt_b[:, cols], op=ALU.add)
+            for j in chunks:
+                nc.scalar.activation(out=t_a[j][:], in_=t_a[j][:], func=ACT.Tanh)
+            for j in chunks:
+                cols = slice(CHUNK * j, CHUNK * (j + 1))
+                o_t = work.tile([P, CHUNK], F32, tag="o", name="o%d" % j)
+                nc.vector.tensor_tensor(out=t_a[j][:], in0=t_a[j][:], in1=hb[:, cols], op=ALU.subtract)
+                nc.vector.tensor_tensor(out=t_a[j][:], in0=t_a[j][:], in1=q_all[:, cols], op=ALU.mult)
+                nc.vector.tensor_tensor(out=o_t[:], in0=t_a[j][:], in1=h_sb[:, cols], op=ALU.add)
+                nc.sync.dma_start(out=out[:, cols], in_=o_t[:])
+
+        for half in range(2):
+            prep_f(half)
+            accs = open_groups("mod", (2 * half, 2 * half + 1))
+            mx_passes("mod", accs, 0, GROUPS)
+            f_side(accs)
+        prep_a(0)
+        prep_a(1)
+        accs = open_groups("tgt", (0, 1))
+        mx_passes("tgt", accs, 0, GROUPS)
+        a_side(accs)
+        for j in (2, 3):
+            accs = open_groups("tgt", (j,))
+            mx_passes("tgt", accs, 0, GROUPS)
+            a_side(accs)

@@ -42,12 +42,14 @@ def tile_ltccell_w_kernel(
     with ExitStack() as ctx:
         keep = ctx.enter_context(tc.tile_pool(name="keep", bufs=1))
         work = ctx.enter_context(tc.tile_pool(name="work", bufs=3))
-        psum = ctx.enter_context(tc.psum_pool(name="psum", bufs=8))
+        psz = ctx.enter_context(tc.psum_pool(name="psz", bufs=2))
+        psab = ctx.enter_context(tc.psum_pool(name="psab", bufs=1))
+        psm = ctx.enter_context(tc.psum_pool(name="psm", bufs=2))
         ctx.enter_context(tc.manual_schedule())
 
         words_mod = keep.tile([P, GROUPS, H_DIM], I32, align_bytes=64)
         words_tgt = keep.tile([P, GROUPS, H_DIM], I32, align_bytes=64)
-        planes = keep.tile([P, 3, H_DIM], U8, align_bytes=64)
+        planes = keep.tile([P, 4, H_DIM], U8, align_bytes=64)
         c_sb = keep.tile([P, K_DIM], BF16, align_bytes=64)
         grouped = keep.tile([P, GROUPS * 512], BF16, align_bytes=64)
         c_codes = keep.tile([P, GROUPS * P], U32, align_bytes=64)
@@ -66,10 +68,9 @@ def tile_ltccell_w_kernel(
         beta = keep.tile([P, 16], F32)
         bmod_b = keep.tile([P, H_DIM], BF16)
         btgt_b = keep.tile([P, H_DIM], BF16)
-        alpha_b = keep.tile([P, H_DIM], F32)
-        beta_b = keep.tile([P, H_DIM], F32)
         hb = keep.tile([P, H_DIM], F32)
         q_all = keep.tile([P, H_DIM], F32)
+        p_all = keep.tile([P, H_DIM], F32)
 
         words = {"mod": words_mod, "tgt": words_tgt}
         src_words = {
@@ -79,14 +80,20 @@ def tile_ltccell_w_kernel(
         h_sb = c_sb[:, I_DIM:K_DIM]
 
         def plane_of(w, g):
-            if w == "mod":
-                return (0, 4 * g) if g < 4 else (1, 4 * (g - 4))
-            return (1, 8 + 4 * g) if g < 2 else (2, 4 * (g - 2))
+            first = 0 if w == "mod" else 2
+            return (first + g // 4, 4 * (g % 4))
 
-        nc.vector.memset(warm[:], 0.0)
-        nc.vector.memset(planes[:].bitcast(I32), 0)
         nc.vector.memset(ltr[:].bitcast(I32), 0)
         nc.vector.memset(rows[:].bitcast(I32), 0)
+        nc.vector.memset(planes[:, 0:2, :].bitcast(I32), 0)
+        nc.vector.memset(warm[:], 0.0)
+        nc.vector.memset(planes[:, 2:4, :].bitcast(I32), 0)
+        with nc.allow_non_contiguous_dma(reason="one bf16 value for each partition"):
+            nc.scalar.dma_start(out=dt_sb[:], in_=time_delta)
+        nc.scalar.dma_start(out=ltr[0:16, :], in_=log_tau.rearrange("(c j) -> c j", c=16))
+        nc.scalar.dma_start(out=rows[0:1, :], in_=b_mod.unsqueeze(0))
+        nc.scalar.dma_start(out=rows[32:33, :], in_=b_tgt.unsqueeze(0))
+        nc.scalar.dma_start(out=rows[64:65, :], in_=bias.unsqueeze(0))
         nc.scalar.activation(out=warm_out[:], in_=warm[:], func=ACT.Exp)
         masks.make_identity(nc, ident_f[:])
         masks.make_identity(nc, ident_b[:])
@@ -105,39 +112,26 @@ def tile_ltccell_w_kernel(
 
         load_planes(0, 0, W_mod_scales[0:4])
         load_planes(1, 0, W_mod_scales[4:6])
-        load_planes(1, 8, W_tgt_scales[0:2])
-        load_planes(2, 0, W_tgt_scales[2:6])
 
-        loads = [
-            ("mod", 0, 2, 0, 1024),
-            ("mod", 2, 4, 0, 1024),
-            ("mod", 4, 6, 0, 1024),
-            ("mod", 0, 2, 1024, 2048),
-            ("mod", 2, 4, 1024, 2048),
-            ("mod", 4, 6, 1024, 2048),
-            ("tgt", 0, 2, 0, 1024),
-            ("tgt", 2, 4, 0, 1024),
-            ("tgt", 4, 6, 0, 1024),
-            ("tgt", 0, 3, 1024, 1536),
-            ("tgt", 3, 6, 1024, 1536),
-            ("tgt", 0, 3, 1536, 2048),
-            ("tgt", 3, 5, 1536, 2048),
-            ("tgt", 5, 6, 1536, 2048),
-        ]
-        for w, g0, g1, n0, n1 in loads:
+        order = (("mod", 0), ("mod", 1), ("mod", 2), ("mod", 3), ("tgt", 0), ("tgt", 1), ("tgt", 2), ("tgt", 3))
+        loads = []
+        for w, j in order:
+            cuts = (0, 3, 5, 6) if (w, j) == order[-1] else (0, 3, 6)
+            for i in range(len(cuts) - 1):
+                loads.append((w, cuts[i], cuts[i + 1], CHUNK * j, CHUNK * (j + 1)))
+        for i, (w, g0, g1, n0, n1) in enumerate(loads):
+            if i == 8:
+                load_planes(2, 0, W_tgt_scales[0:4])
+                load_planes(3, 0, W_tgt_scales[4:6])
             nc.sync.dma_start(out=words[w][:, g0:g1, n0:n1], in_=src_words[w][:, g0:g1, n0:n1])
-
-        nc.gpsimd.dma_start(out=ltr[0:16, :], in_=log_tau.rearrange("(c j) -> c j", c=16))
-        nc.gpsimd.dma_start(out=rows[0:1, :], in_=b_mod.unsqueeze(0))
-        with nc.allow_non_contiguous_dma(reason="one bf16 value for each partition"):
-            nc.gpsimd.dma_start(out=dt_sb[:], in_=time_delta)
-        nc.gpsimd.dma_start(out=rows[32:33, :], in_=b_tgt.unsqueeze(0))
-        nc.gpsimd.dma_start(out=rows[64:65, :], in_=bias.unsqueeze(0))
 
         c32 = c_sb[:].bitcast(F32)
         g32 = grouped[:].bitcast(F32).rearrange("p (g t u) -> p g t u", g=GROUPS, t=P, u=2)
         for b in range(3):
-            xt = psum.tile([P, 2, 2, P], F32, tag="bank", name="xt%d" % b)
+            if b < 2:
+                xt = psm.tile([P, 2, 2, P], F32, tag="misc", name="xt%d" % b)
+            else:
+                xt = psab.tile([P, 2, 2, P], F32, tag="be", name="xt%d" % b)
             for gi in range(2):
                 g = 2 * b + gi
                 for u in range(2):
@@ -158,7 +152,7 @@ def tile_ltccell_w_kernel(
             in_=grouped[:, 1024:3072],
         )
 
-        ps_lt = psum.tile([P, P], BF16, tag="bank", name="ps_lt")
+        ps_lt = psab.tile([P, P], BF16, tag="al", name="ps_lt")
         nc.tensor.transpose(ps_lt[:], ltr[:], ident_b[:])
         nc.scalar.activation(out=tau[:], in_=ps_lt[:, 0:16], func=ACT.Exp)
         nc.vector.tensor_scalar(out=ndt[:], in0=dt_sb[:], scalar1=-1.0, scalar2=None, op0=ALU.mult)
@@ -169,7 +163,7 @@ def tile_ltccell_w_kernel(
         )
 
         def spread_row(row, half, name):
-            ps = psum.tile([P, 1024], BF16, tag="bank", name=name)
+            ps = psm.tile([P, 1024], BF16, tag="misc", name=name)
             for i in range(2):
                 n0 = 1024 * half + 512 * i
                 nc.tensor.matmul(
@@ -181,8 +175,8 @@ def tile_ltccell_w_kernel(
                 )
             return ps
 
-        def spread_small(small, j, name):
-            ps = psum.tile([P, CHUNK], F32, tag="bank", name=name)
+        def spread_small(small, j, tag):
+            ps = psab.tile([P, CHUNK], F32, tag=tag, name="%s%d" % (tag, j))
             for i in range(4):
                 c = 4 * j + i
                 nc.tensor.transpose(
@@ -190,15 +184,9 @@ def tile_ltccell_w_kernel(
                 )
             return ps
 
-        def prep_f(half):
+        def prep_bmod(half):
             ps = spread_row(0, half, "ps_bmod%d" % half)
             nc.scalar.copy(out=bmod_b[:, 1024 * half : 1024 * (half + 1)], in_=ps[:])
-            for j in (2 * half, 2 * half + 1):
-                cols = slice(CHUNK * j, CHUNK * (j + 1))
-                ps_b = spread_small(beta, j, "ps_beta%d" % j)
-                nc.vector.tensor_copy(out=beta_b[:, cols], in_=ps_b[:])
-                ps_a = spread_small(alpha, j, "ps_alpha%d" % j)
-                nc.scalar.copy(out=alpha_b[:, cols], in_=ps_a[:])
 
         def prep_a(half):
             cols = slice(1024 * half, 1024 * (half + 1))
@@ -207,92 +195,87 @@ def tile_ltccell_w_kernel(
             ps2 = spread_row(64, half, "ps_bias%d" % half)
             nc.vector.tensor_tensor(out=hb[:, cols], in0=h_sb[:, cols], in1=ps2[:], op=ALU.subtract)
 
-        def mx_passes(w, accs, g0, g1):
-            for g in range(g0, g1):
+        def cols_of(j):
+            return slice(CHUNK * j, CHUNK * (j + 1))
+
+        def mx_passes(w, j):
+            acc = psz.tile([P, CHUNK], F32, tag="z" + w, name="z_%s%d" % (w, j))
+            for g in range(GROUPS):
                 slot, k = plane_of(w, g)
-                for j in sorted(accs):
-                    cols = slice(CHUNK * j, CHUNK * (j + 1))
-                    nc.tensor.matmul_mx(
-                        out=accs[j][:],
-                        lhsT=c_codes[:, P * g : P * (g + 1)].bitcast(FP8X4),
-                        lhsT_scale=c_scales[:, P * g : P * (g + 1)],
-                        rhs=words[w][:, g, cols].bitcast(FP8X4),
-                        rhs_scale=planes[k:P, slot, cols],
-                        start=(g == 0),
-                        stop=(g == GROUPS - 1),
-                    )
-
-        def open_groups(w, chunks):
-            accs = {}
-            for j in chunks:
-                acc = psum.tile([P, CHUNK], F32, tag="bank", name="z_%s%d" % (w, j))
-                accs[j] = acc
-            return accs
-
-        def f_side(accs):
-            chunks = sorted(accs)
-            t_u = {}
-            t_a1 = {}
-            t_q = {}
-            t_r = {}
-            for j in chunks:
-                cols = slice(CHUNK * j, CHUNK * (j + 1))
-                u_t = work.tile([P, CHUNK], F32, tag="u", name="u%d" % j)
-                t_u[j] = u_t
-                nc.vector.tensor_tensor(out=u_t[:], in0=accs[j][:], in1=bmod_b[:, cols], op=ALU.add)
-            for j in chunks:
-                nc.scalar.activation(out=t_u[j][:], in_=t_u[j][:], func=ACT.Abs)
-                nc.scalar.activation(out=t_u[j][:], in_=t_u[j][:], func=ACT.Tanh)
-            for j in chunks:
-                cols = slice(CHUNK * j, CHUNK * (j + 1))
-                a1_t = work.tile([P, CHUNK], F32, tag="a1", name="a1_%d" % j)
-                r_t = work.tile([P, CHUNK], F32, tag="r", name="r%d" % j)
-                t_a1[j] = a1_t
-                t_r[j] = r_t
-                nc.vector.tensor_tensor(out=a1_t[:], in0=t_u[j][:], in1=beta_b[:, cols], op=ALU.mult)
-                nc.vector.tensor_tensor(out=r_t[:], in0=a1_t[:], in1=alpha_b[:, cols], op=ALU.add)
-            for j in chunks:
-                q_t = work.tile([P, CHUNK], F32, tag="q", name="q%d" % j)
-                t_q[j] = q_t
-                nc.scalar.activation(out=q_t[:], in_=t_a1[j][:], func=ACT.Copy, bias=1.0, scale=-EPS)
-            for j in chunks:
-                nc.vector.tensor_tensor(out=t_r[j][:], in0=t_r[j][:], in1=t_q[j][:], op=ALU.mult)
-            for j in chunks:
-                cols = slice(CHUNK * j, CHUNK * (j + 1))
-                nc.scalar.activation(out=t_r[j][:], in_=t_r[j][:], func=ACT.Exp, scale=ndt[:, 0:1])
-                nc.scalar.activation(
-                    out=q_all[:, cols], in_=t_r[j][:], func=ACT.Copy, bias=1.0, scale=-1.0
+                nc.tensor.matmul_mx(
+                    out=acc[:],
+                    lhsT=c_codes[:, P * g : P * (g + 1)].bitcast(FP8X4),
+                    lhsT_scale=c_scales[:, P * g : P * (g + 1)],
+                    rhs=words[w][:, g, cols_of(j)].bitcast(FP8X4),
+                    rhs_scale=planes[k:P, slot, cols_of(j)],
+                    start=(g == 0),
+                    stop=(g == GROUPS - 1),
                 )
+            return acc
 
-        def a_side(accs):
-            chunks = sorted(accs)
-            t_a = {}
-            for j in chunks:
-                cols = slice(CHUNK * j, CHUNK * (j + 1))
-                a_t = work.tile([P, CHUNK], F32, tag="a", name="a%d" % j)
-                t_a[j] = a_t
-                nc.vector.tensor_tensor(out=a_t[:], in0=accs[j][:], in1=btgt_b[:, cols], op=ALU.add)
-            for j in chunks:
-                nc.scalar.activation(out=t_a[j][:], in_=t_a[j][:], func=ACT.Tanh)
-            for j in chunks:
-                cols = slice(CHUNK * j, CHUNK * (j + 1))
-                o_t = work.tile([P, CHUNK], F32, tag="o", name="o%d" % j)
-                nc.vector.tensor_tensor(out=t_a[j][:], in0=t_a[j][:], in1=hb[:, cols], op=ALU.subtract)
-                nc.vector.tensor_tensor(out=t_a[j][:], in0=t_a[j][:], in1=q_all[:, cols], op=ALU.mult)
-                nc.vector.tensor_tensor(out=o_t[:], in0=t_a[j][:], in1=h_sb[:, cols], op=ALU.add)
-                nc.sync.dma_start(out=out[:, cols], in_=o_t[:])
+        live = {}
+        LATE = (2, 3)
 
-        for half in range(2):
-            prep_f(half)
-            accs = open_groups("mod", (2 * half, 2 * half + 1))
-            mx_passes("mod", accs, 0, GROUPS)
-            f_side(accs)
-        prep_a(0)
-        prep_a(1)
-        accs = open_groups("tgt", (0, 1))
-        mx_passes("tgt", accs, 0, GROUPS)
-        a_side(accs)
-        for j in (2, 3):
-            accs = open_groups("tgt", (j,))
-            mx_passes("tgt", accs, 0, GROUPS)
-            a_side(accs)
+        def first_stage(w, j, acc):
+            b_b = bmod_b if w == "mod" else btgt_b
+            z_t = work.tile([P, CHUNK], F32, tag="s" + w, name="s_%s%d" % (w, j))
+            live[(w, j)] = z_t
+            nc.vector.tensor_tensor(out=z_t[:], in0=acc[:], in1=b_b[:, cols_of(j)], op=ALU.add)
+            if w == "mod":
+                nc.scalar.activation(out=z_t[:], in_=z_t[:], func=ACT.Abs)
+            nc.scalar.activation(out=z_t[:], in_=z_t[:], func=ACT.Tanh)
+
+        def rest_mod(j, ps_beta, ps_alpha):
+            u_t = live[("mod", j)]
+            a1_t = work.tile([P, CHUNK], F32, tag="a1", name="a1_%d" % j)
+            r_t = work.tile([P, CHUNK], F32, tag="r", name="r%d" % j)
+            q_t = work.tile([P, CHUNK], F32, tag="q", name="q%d" % j)
+            nc.vector.tensor_tensor(out=a1_t[:], in0=u_t[:], in1=ps_beta[:], op=ALU.mult)
+            nc.vector.tensor_tensor(out=r_t[:], in0=a1_t[:], in1=ps_alpha[:], op=ALU.add)
+            nc.vector.tensor_scalar(
+                out=q_t[:], in0=a1_t[:], scalar1=-EPS, scalar2=1.0, op0=ALU.mult, op1=ALU.add
+            )
+            nc.vector.tensor_tensor(out=r_t[:], in0=r_t[:], in1=q_t[:], op=ALU.mult)
+            nc.scalar.activation(out=r_t[:], in_=r_t[:], func=ACT.Exp, scale=ndt[:, 0:1])
+            nc.scalar.activation(
+                out=q_all[:, cols_of(j)], in_=r_t[:], func=ACT.Copy, bias=1.0, scale=-1.0
+            )
+
+        def blend_ahead(j):
+            cols = cols_of(j)
+            nc.vector.tensor_tensor(out=p_all[:, cols], in0=q_all[:, cols], in1=hb[:, cols], op=ALU.mult)
+            nc.vector.tensor_tensor(out=p_all[:, cols], in0=h_sb[:, cols], in1=p_all[:, cols], op=ALU.subtract)
+
+        def rest_tgt(j):
+            cols = cols_of(j)
+            a_t = live[("tgt", j)]
+            o_t = work.tile([P, CHUNK], F32, tag="o", name="o%d" % j)
+            if j in LATE:
+                nc.vector.tensor_tensor(out=a_t[:], in0=a_t[:], in1=q_all[:, cols], op=ALU.mult)
+                nc.vector.tensor_tensor(out=o_t[:], in0=a_t[:], in1=p_all[:, cols], op=ALU.add)
+            else:
+                nc.vector.tensor_tensor(out=a_t[:], in0=a_t[:], in1=hb[:, cols], op=ALU.subtract)
+                nc.vector.tensor_tensor(out=a_t[:], in0=a_t[:], in1=q_all[:, cols], op=ALU.mult)
+                nc.vector.tensor_tensor(out=o_t[:], in0=a_t[:], in1=h_sb[:, cols], op=ALU.add)
+            nc.sync.dma_start(out=out[:, cols], in_=o_t[:])
+
+        prep_bmod(0)
+        prep_bmod(1)
+        preps = {1: 0, 2: 1}
+        for k in range(len(order) + 1):
+            before = order[k - 1] if k > 0 else None
+            if k < len(order):
+                w, j = order[k]
+                acc = mx_passes(w, j)
+                first_stage(w, j, acc)
+            if before is not None:
+                if before[0] == "mod":
+                    ps_beta = spread_small(beta, before[1], "be")
+                    ps_alpha = spread_small(alpha, before[1], "al")
+                    rest_mod(before[1], ps_beta, ps_alpha)
+                else:
+                    rest_tgt(before[1])
+            if k in preps:
+                prep_a(preps[k])
+            if k >= 2 and order[k - 2][0] == "mod" and order[k - 2][1] in LATE:
+                blend_ahead(order[k - 2][1])

@@ -60,7 +60,6 @@ def tile_ltccell_w_kernel(
         ident_b = keep.tile([P, P], BF16)
         warm = keep.tile([P, 1], F32)
         warm_out = keep.tile([P, 1], F32)
-        dt_sb = keep.tile([P, 1], BF16)
         ndt = keep.tile([P, 1], F32)
         tau = keep.tile([P, 16], F32)
         tau_eps = keep.tile([P, 16], F32)
@@ -84,46 +83,46 @@ def tile_ltccell_w_kernel(
             return (first + g // 4, 4 * (g % 4))
 
         nc.vector.memset(ltr[:].bitcast(I32), 0)
+        nc.vector.memset(planes[:, 0:1, :].bitcast(I32), 0)
         nc.vector.memset(rows[:].bitcast(I32), 0)
-        nc.vector.memset(planes[:, 0:2, :].bitcast(I32), 0)
+        nc.vector.memset(planes[:, 1:2, :].bitcast(I32), 0)
         nc.vector.memset(warm[:], 0.0)
         nc.vector.memset(planes[:, 2:4, :].bitcast(I32), 0)
-        with nc.allow_non_contiguous_dma(reason="one bf16 value for each partition"):
-            nc.scalar.dma_start(out=dt_sb[:], in_=time_delta)
-        nc.scalar.dma_start(out=ltr[0:16, :], in_=log_tau.rearrange("(c j) -> c j", c=16))
-        nc.scalar.dma_start(out=rows[0:1, :], in_=b_mod.unsqueeze(0))
-        nc.scalar.dma_start(out=rows[32:33, :], in_=b_tgt.unsqueeze(0))
-        nc.scalar.dma_start(out=rows[64:65, :], in_=bias.unsqueeze(0))
-        nc.scalar.activation(out=warm_out[:], in_=warm[:], func=ACT.Exp)
         masks.make_identity(nc, ident_f[:])
         masks.make_identity(nc, ident_b[:])
 
-        nc.sync.dma_start(out=c_sb[:, 0:I_DIM], in_=x)
-        nc.sync.dma_start(out=c_sb[:, I_DIM:K_DIM], in_=h)
-
-        def load_planes(slot, first_row, src):
+        def load_planes(queue, view, slot, src):
             n_rows = 4 * src.shape[0]
             for q in range(4):
-                lo = 32 * q + first_row
-                nc.sync.dma_start(
-                    out=planes[lo : lo + n_rows, slot, :].bitcast(I32),
-                    in_=src[:, 4 * q : 4 * q + 4, :].bitcast(I32),
+                queue.dma_start(
+                    out=planes[32 * q : 32 * q + n_rows, slot, :].bitcast(view),
+                    in_=src[:, 4 * q : 4 * q + 4, :].bitcast(view),
                 )
 
-        load_planes(0, 0, W_mod_scales[0:4])
-        load_planes(1, 0, W_mod_scales[4:6])
+        def load_words(w, j, g0, g1):
+            cols = slice(CHUNK * j, CHUNK * (j + 1))
+            nc.sync.dma_start(out=words[w][:, g0:g1, cols], in_=src_words[w][:, g0:g1, cols])
 
         order = (("mod", 0), ("mod", 1), ("mod", 2), ("mod", 3), ("tgt", 0), ("tgt", 1), ("tgt", 2), ("tgt", 3))
-        loads = []
-        for w, j in order:
+
+        nc.sync.dma_start(out=c_sb[:, 0:I_DIM], in_=x)
+        nc.sync.dma_start(out=c_sb[:, I_DIM:K_DIM], in_=h)
+        nc.scalar.dma_start(out=ltr[0:16, :], in_=log_tau.rearrange("(c j) -> c j", c=16))
+        nc.scalar.dma_start(out=ltr[16:17, :], in_=time_delta.rearrange("p o -> o p"))
+        load_planes(nc.sync, I32, 0, W_mod_scales[0:4])
+        nc.scalar.dma_start(out=rows[0:1, :], in_=b_mod.unsqueeze(0))
+        nc.scalar.dma_start(out=rows[64:65, :], in_=bias.unsqueeze(0))
+        load_words("mod", 0, 0, 3)
+        load_planes(nc.sync, I32, 1, W_mod_scales[4:6])
+        load_words("mod", 0, 3, 6)
+        nc.scalar.dma_start(out=rows[32:33, :], in_=b_tgt.unsqueeze(0))
+        nc.scalar.activation(out=warm_out[:], in_=warm[:], func=ACT.Exp)
+        load_planes(nc.gpsimd, F32, 2, W_tgt_scales[0:4])
+        load_planes(nc.gpsimd, F32, 3, W_tgt_scales[4:6])
+        for w, j in order[1:]:
             cuts = (0, 3, 5, 6) if (w, j) == order[-1] else (0, 3, 6)
             for i in range(len(cuts) - 1):
-                loads.append((w, cuts[i], cuts[i + 1], CHUNK * j, CHUNK * (j + 1)))
-        for i, (w, g0, g1, n0, n1) in enumerate(loads):
-            if i == 8:
-                load_planes(2, 0, W_tgt_scales[0:4])
-                load_planes(3, 0, W_tgt_scales[4:6])
-            nc.sync.dma_start(out=words[w][:, g0:g1, n0:n1], in_=src_words[w][:, g0:g1, n0:n1])
+                load_words(w, j, cuts[i], cuts[i + 1])
 
         c32 = c_sb[:].bitcast(F32)
         g32 = grouped[:].bitcast(F32).rearrange("p (g t u) -> p g t u", g=GROUPS, t=P, u=2)
@@ -155,7 +154,9 @@ def tile_ltccell_w_kernel(
         ps_lt = psab.tile([P, P], BF16, tag="al", name="ps_lt")
         nc.tensor.transpose(ps_lt[:], ltr[:], ident_b[:])
         nc.scalar.activation(out=tau[:], in_=ps_lt[:, 0:16], func=ACT.Exp)
-        nc.vector.tensor_scalar(out=ndt[:], in0=dt_sb[:], scalar1=-1.0, scalar2=None, op0=ALU.mult)
+        nc.vector.tensor_scalar(
+            out=ndt[:], in0=ps_lt[:, 16:17], scalar1=-1.0, scalar2=None, op0=ALU.mult
+        )
         nc.vector.tensor_scalar(out=tau_eps[:], in0=tau[:], scalar1=EPS, scalar2=None, op0=ALU.add)
         nc.vector.reciprocal(out=alpha[:], in_=tau_eps[:])
         nc.vector.tensor_scalar(
@@ -188,12 +189,14 @@ def tile_ltccell_w_kernel(
             ps = spread_row(0, half, "ps_bmod%d" % half)
             nc.scalar.copy(out=bmod_b[:, 1024 * half : 1024 * (half + 1)], in_=ps[:])
 
-        def prep_a(half):
-            cols = slice(1024 * half, 1024 * (half + 1))
+        def prep_btgt(half):
             ps = spread_row(32, half, "ps_btgt%d" % half)
-            nc.scalar.copy(out=btgt_b[:, cols], in_=ps[:])
-            ps2 = spread_row(64, half, "ps_bias%d" % half)
-            nc.vector.tensor_tensor(out=hb[:, cols], in0=h_sb[:, cols], in1=ps2[:], op=ALU.subtract)
+            nc.scalar.copy(out=btgt_b[:, 1024 * half : 1024 * (half + 1)], in_=ps[:])
+
+        def prep_hb(half):
+            cols = slice(1024 * half, 1024 * (half + 1))
+            ps = spread_row(64, half, "ps_bias%d" % half)
+            nc.vector.tensor_tensor(out=hb[:, cols], in0=h_sb[:, cols], in1=ps[:], op=ALU.subtract)
 
         def cols_of(j):
             return slice(CHUNK * j, CHUNK * (j + 1))
@@ -260,7 +263,9 @@ def tile_ltccell_w_kernel(
             nc.sync.dma_start(out=out[:, cols], in_=o_t[:])
 
         prep_bmod(0)
+        prep_hb(0)
         prep_bmod(1)
+        prep_hb(1)
         preps = {1: 0, 2: 1}
         for k in range(len(order) + 1):
             before = order[k - 1] if k > 0 else None
@@ -276,6 +281,6 @@ def tile_ltccell_w_kernel(
                 else:
                     rest_tgt(before[1])
             if k in preps:
-                prep_a(preps[k])
+                prep_btgt(preps[k])
             if k >= 2 and order[k - 2][0] == "mod" and order[k - 2][1] in LATE:
                 blend_ahead(order[k - 2][1])

@@ -82,14 +82,13 @@ def tile_ltccell_w_kernel(
             first = 0 if w == "mod" else 2
             return (first + g // 4, 4 * (g % 4))
 
+        nc.vector.memset(planes[:, 0:2, :].bitcast(I32), 0)
         nc.vector.memset(ltr[:].bitcast(I32), 0)
-        nc.vector.memset(planes[:, 0:1, :].bitcast(I32), 0)
         nc.vector.memset(rows[:].bitcast(I32), 0)
-        nc.vector.memset(planes[:, 1:2, :].bitcast(I32), 0)
         nc.vector.memset(warm[:], 0.0)
-        nc.vector.memset(planes[:, 2:4, :].bitcast(I32), 0)
         masks.make_identity(nc, ident_f[:])
-        masks.make_identity(nc, ident_b[:])
+        nc.vector.tensor_copy(out=ident_b[:], in_=ident_f[:])
+        nc.vector.memset(planes[:, 2:4, :].bitcast(I32), 0)
 
         def load_planes(queue, view, slot, src):
             n_rows = 4 * src.shape[0]
@@ -109,14 +108,14 @@ def tile_ltccell_w_kernel(
         nc.sync.dma_start(out=c_sb[:, I_DIM:K_DIM], in_=h)
         nc.scalar.dma_start(out=ltr[0:16, :], in_=log_tau.rearrange("(c j) -> c j", c=16))
         nc.scalar.dma_start(out=ltr[16:17, :], in_=time_delta.rearrange("p o -> o p"))
-        load_planes(nc.sync, I32, 0, W_mod_scales[0:4])
         nc.scalar.dma_start(out=rows[0:1, :], in_=b_mod.unsqueeze(0))
         nc.scalar.dma_start(out=rows[64:65, :], in_=bias.unsqueeze(0))
         load_words("mod", 0, 0, 3)
-        load_planes(nc.sync, I32, 1, W_mod_scales[4:6])
         load_words("mod", 0, 3, 6)
         nc.scalar.dma_start(out=rows[32:33, :], in_=b_tgt.unsqueeze(0))
         nc.scalar.activation(out=warm_out[:], in_=warm[:], func=ACT.Exp)
+        load_planes(nc.gpsimd, F32, 0, W_mod_scales[0:4])
+        load_planes(nc.gpsimd, F32, 1, W_mod_scales[4:6])
         load_planes(nc.gpsimd, F32, 2, W_tgt_scales[0:4])
         load_planes(nc.gpsimd, F32, 3, W_tgt_scales[4:6])
         for w, j in order[1:]:

@@ -82,13 +82,14 @@ def tile_ltccell_w_kernel(
             first = 0 if w == "mod" else 2
             return (first + g // 4, 4 * (g % 4))
 
-        nc.vector.memset(planes[:, 0:2, :].bitcast(I32), 0)
         nc.vector.memset(ltr[:].bitcast(I32), 0)
+        nc.vector.memset(planes[:, 0:1, :].bitcast(I32), 0)
         nc.vector.memset(rows[:].bitcast(I32), 0)
+        nc.vector.memset(planes[:, 1:2, :].bitcast(I32), 0)
         nc.vector.memset(warm[:], 0.0)
-        masks.make_identity(nc, ident_f[:])
-        nc.vector.tensor_copy(out=ident_b[:], in_=ident_f[:])
         nc.vector.memset(planes[:, 2:4, :].bitcast(I32), 0)
+        masks.make_identity(nc, ident_f[:])
+        masks.make_identity(nc, ident_b[:])
 
         def load_planes(queue, view, slot, src):
             n_rows = 4 * src.shape[0]
@@ -108,14 +109,14 @@ def tile_ltccell_w_kernel(
         nc.sync.dma_start(out=c_sb[:, I_DIM:K_DIM], in_=h)
         nc.scalar.dma_start(out=ltr[0:16, :], in_=log_tau.rearrange("(c j) -> c j", c=16))
         nc.scalar.dma_start(out=ltr[16:17, :], in_=time_delta.rearrange("p o -> o p"))
+        load_planes(nc.sync, I32, 0, W_mod_scales[0:4])
         nc.scalar.dma_start(out=rows[0:1, :], in_=b_mod.unsqueeze(0))
         nc.scalar.dma_start(out=rows[64:65, :], in_=bias.unsqueeze(0))
         load_words("mod", 0, 0, 3)
+        load_planes(nc.sync, I32, 1, W_mod_scales[4:6])
         load_words("mod", 0, 3, 6)
         nc.scalar.dma_start(out=rows[32:33, :], in_=b_tgt.unsqueeze(0))
         nc.scalar.activation(out=warm_out[:], in_=warm[:], func=ACT.Exp)
-        load_planes(nc.gpsimd, F32, 0, W_mod_scales[0:4])
-        load_planes(nc.gpsimd, F32, 1, W_mod_scales[4:6])
         load_planes(nc.gpsimd, F32, 2, W_tgt_scales[0:4])
         load_planes(nc.gpsimd, F32, 3, W_tgt_scales[4:6])
         for w, j in order[1:]:
@@ -216,70 +217,95 @@ def tile_ltccell_w_kernel(
             return acc
 
         live = {}
-        LATE = (2, 3)
 
-        def first_stage(w, j, acc):
+        def pieces_of(w, j):
+            n = 2 if (w, j) == order[-1] else 1
+            width = CHUNK // n
+            return [(width * i, width * (i + 1)) for i in range(n)]
+
+        def bias_add(w, j, acc):
             b_b = bmod_b if w == "mod" else btgt_b
             z_t = work.tile([P, CHUNK], F32, tag="s" + w, name="s_%s%d" % (w, j))
             live[(w, j)] = z_t
-            nc.vector.tensor_tensor(out=z_t[:], in0=acc[:], in1=b_b[:, cols_of(j)], op=ALU.add)
-            if w == "mod":
-                nc.scalar.activation(out=z_t[:], in_=z_t[:], func=ACT.Abs)
-            nc.scalar.activation(out=z_t[:], in_=z_t[:], func=ACT.Tanh)
+            for lo, hi in pieces_of(w, j):
+                nc.vector.tensor_tensor(
+                    out=z_t[:, lo:hi],
+                    in0=acc[:, lo:hi],
+                    in1=b_b[:, CHUNK * j + lo : CHUNK * j + hi],
+                    op=ALU.add,
+                )
+            for lo, hi in pieces_of(w, j):
+                if w == "mod":
+                    nc.scalar.activation(out=z_t[:, lo:hi], in_=z_t[:, lo:hi], func=ACT.Abs)
+                nc.scalar.activation(out=z_t[:, lo:hi], in_=z_t[:, lo:hi], func=ACT.Tanh)
 
-        def rest_mod(j, ps_beta, ps_alpha):
-            u_t = live[("mod", j)]
+        def mod_a(j):
             a1_t = work.tile([P, CHUNK], F32, tag="a1", name="a1_%d" % j)
-            r_t = work.tile([P, CHUNK], F32, tag="r", name="r%d" % j)
             q_t = work.tile([P, CHUNK], F32, tag="q", name="q%d" % j)
-            nc.vector.tensor_tensor(out=a1_t[:], in0=u_t[:], in1=ps_beta[:], op=ALU.mult)
-            nc.vector.tensor_tensor(out=r_t[:], in0=a1_t[:], in1=ps_alpha[:], op=ALU.add)
-            nc.vector.tensor_scalar(
-                out=q_t[:], in0=a1_t[:], scalar1=-EPS, scalar2=1.0, op0=ALU.mult, op1=ALU.add
-            )
-            nc.vector.tensor_tensor(out=r_t[:], in0=r_t[:], in1=q_t[:], op=ALU.mult)
+            live[("a1", j)] = a1_t
+            live[("q", j)] = q_t
+            nc.vector.tensor_tensor(out=a1_t[:], in0=live[("mod", j)][:], in1=live[("be", j)][:], op=ALU.mult)
+            nc.scalar.activation(out=q_t[:], in_=a1_t[:], func=ACT.Copy, bias=1.0, scale=-EPS)
+
+        def mod_b(j):
+            r_t = work.tile([P, CHUNK], F32, tag="r", name="r%d" % j)
+            live[("r", j)] = r_t
+            nc.vector.tensor_tensor(out=r_t[:], in0=live[("a1", j)][:], in1=live[("al", j)][:], op=ALU.add)
+
+        def mod_c(j):
+            cols = cols_of(j)
+            r_t = live[("r", j)]
+            nc.vector.tensor_tensor(out=r_t[:], in0=r_t[:], in1=live[("q", j)][:], op=ALU.mult)
             nc.scalar.activation(out=r_t[:], in_=r_t[:], func=ACT.Exp, scale=ndt[:, 0:1])
-            nc.scalar.activation(
-                out=q_all[:, cols_of(j)], in_=r_t[:], func=ACT.Copy, bias=1.0, scale=-1.0
-            )
+            nc.scalar.activation(out=q_all[:, cols], in_=r_t[:], func=ACT.Copy, bias=1.0, scale=-1.0)
+            nc.gpsimd.tensor_tensor(out=p_all[:, cols], in0=q_all[:, cols], in1=hb[:, cols], op=ALU.mult)
+            nc.gpsimd.tensor_tensor(out=p_all[:, cols], in0=h_sb[:, cols], in1=p_all[:, cols], op=ALU.subtract)
 
-        def blend_ahead(j):
-            cols = cols_of(j)
-            nc.vector.tensor_tensor(out=p_all[:, cols], in0=q_all[:, cols], in1=hb[:, cols], op=ALU.mult)
-            nc.vector.tensor_tensor(out=p_all[:, cols], in0=h_sb[:, cols], in1=p_all[:, cols], op=ALU.subtract)
-
-        def rest_tgt(j):
-            cols = cols_of(j)
+        def tgt_a(j):
             a_t = live[("tgt", j)]
+            for lo, hi in pieces_of("tgt", j):
+                nc.vector.tensor_tensor(
+                    out=a_t[:, lo:hi],
+                    in0=a_t[:, lo:hi],
+                    in1=q_all[:, CHUNK * j + lo : CHUNK * j + hi],
+                    op=ALU.mult,
+                )
+
+        def tgt_b(j):
             o_t = work.tile([P, CHUNK], F32, tag="o", name="o%d" % j)
-            if j in LATE:
-                nc.vector.tensor_tensor(out=a_t[:], in0=a_t[:], in1=q_all[:, cols], op=ALU.mult)
-                nc.vector.tensor_tensor(out=o_t[:], in0=a_t[:], in1=p_all[:, cols], op=ALU.add)
-            else:
-                nc.vector.tensor_tensor(out=a_t[:], in0=a_t[:], in1=hb[:, cols], op=ALU.subtract)
-                nc.vector.tensor_tensor(out=a_t[:], in0=a_t[:], in1=q_all[:, cols], op=ALU.mult)
-                nc.vector.tensor_tensor(out=o_t[:], in0=a_t[:], in1=h_sb[:, cols], op=ALU.add)
-            nc.sync.dma_start(out=out[:, cols], in_=o_t[:])
+            for lo, hi in pieces_of("tgt", j):
+                cols = slice(CHUNK * j + lo, CHUNK * j + hi)
+                nc.vector.tensor_tensor(
+                    out=o_t[:, lo:hi], in0=live[("tgt", j)][:, lo:hi], in1=p_all[:, cols], op=ALU.add
+                )
+                nc.sync.dma_start(out=out[:, cols], in_=o_t[:, lo:hi])
 
         prep_bmod(0)
         prep_hb(0)
         prep_bmod(1)
         prep_hb(1)
         preps = {1: 0, 2: 1}
-        for k in range(len(order) + 1):
-            before = order[k - 1] if k > 0 else None
-            if k < len(order):
-                w, j = order[k]
-                acc = mx_passes(w, j)
-                first_stage(w, j, acc)
-            if before is not None:
-                if before[0] == "mod":
-                    ps_beta = spread_small(beta, before[1], "be")
-                    ps_alpha = spread_small(alpha, before[1], "al")
-                    rest_mod(before[1], ps_beta, ps_alpha)
+        n_events = len(order)
+        for k in range(n_events + 2):
+            acc = None
+            if k < n_events:
+                acc = mx_passes(order[k][0], order[k][1])
+            if 2 <= k and order[k - 2][0] == "mod":
+                mod_c(order[k - 2][1])
+            if 1 <= k <= n_events:
+                if order[k - 1][0] == "mod":
+                    mod_a(order[k - 1][1])
                 else:
-                    rest_tgt(before[1])
+                    tgt_a(order[k - 1][1])
+            if k < n_events:
+                bias_add(order[k][0], order[k][1], acc)
+            if 1 <= k <= n_events:
+                if order[k - 1][0] == "mod":
+                    mod_b(order[k - 1][1])
+                else:
+                    tgt_b(order[k - 1][1])
+            if k < n_events and order[k][0] == "mod":
+                live[("be", order[k][1])] = spread_small(beta, order[k][1], "be")
+                live[("al", order[k][1])] = spread_small(alpha, order[k][1], "al")
             if k in preps:
                 prep_btgt(preps[k])
-            if k >= 2 and order[k - 2][0] == "mod" and order[k - 2][1] in LATE:
-                blend_ahead(order[k - 2][1])

@@ -17,8 +17,12 @@ I_DIM = 1024
 H_DIM = 2048
 K_DIM = I_DIM + H_DIM
 GROUPS = K_DIM // 512
-CHUNK = 512
+BLOCKS = H_DIM // P
+PER_CHUNK = 4
+CHUNK = PER_CHUNK * P
+CHUNKS = H_DIM // CHUNK
 EPS = 1e-6
+INV_EPS = 1e6
 
 FLOPS = 2 * P * K_DIM * 2 * H_DIM
 
@@ -42,9 +46,8 @@ def tile_ltccell_w_kernel(
     with ExitStack() as ctx:
         keep = ctx.enter_context(tc.tile_pool(name="keep", bufs=1))
         work = ctx.enter_context(tc.tile_pool(name="work", bufs=3))
-        psz = ctx.enter_context(tc.psum_pool(name="psz", bufs=2))
-        psab = ctx.enter_context(tc.psum_pool(name="psab", bufs=1))
-        psm = ctx.enter_context(tc.psum_pool(name="psm", bufs=2))
+        psz = ctx.enter_context(tc.psum_pool(name="psz", bufs=4))
+        pst = ctx.enter_context(tc.psum_pool(name="pst", bufs=4))
         ctx.enter_context(tc.manual_schedule())
 
         words_mod = keep.tile([P, GROUPS, H_DIM], I32, align_bytes=64)
@@ -54,22 +57,19 @@ def tile_ltccell_w_kernel(
         grouped = keep.tile([P, GROUPS * 512], BF16, align_bytes=64)
         c_codes = keep.tile([P, GROUPS * P], U32, align_bytes=64)
         c_scales = keep.tile([P, GROUPS * P], U8, align_bytes=64)
-        rows = keep.tile([P, H_DIM], BF16)
-        ltr = keep.tile([P, P], BF16)
+        vec_rows = keep.tile([P, P], BF16)
+        vec_cols = keep.tile([P, 64], F32)
+        dt_all = keep.tile([P, P], F32)
         ident_f = keep.tile([P, P], F32)
         ident_b = keep.tile([P, P], BF16)
         warm = keep.tile([P, 1], F32)
         warm_out = keep.tile([P, 1], F32)
-        ndt = keep.tile([P, 1], F32)
-        tau = keep.tile([P, 16], F32)
-        tau_eps = keep.tile([P, 16], F32)
-        alpha = keep.tile([P, 16], F32)
-        beta = keep.tile([P, 16], F32)
-        bmod_b = keep.tile([P, H_DIM], BF16)
-        btgt_b = keep.tile([P, H_DIM], BF16)
-        hb = keep.tile([P, H_DIM], F32)
+        r_tau = keep.tile([P, BLOCKS], F32)
+        shift = keep.tile([P, BLOCKS], F32)
+        damp = keep.tile([P, BLOCKS], F32)
+        rate = keep.tile([P, BLOCKS], F32)
         q_all = keep.tile([P, H_DIM], F32)
-        p_all = keep.tile([P, H_DIM], F32)
+        dh_all = keep.tile([P, H_DIM], F32)
 
         words = {"mod": words_mod, "tgt": words_tgt}
         src_words = {
@@ -77,66 +77,58 @@ def tile_ltccell_w_kernel(
             "tgt": W_tgt_words.rearrange("g p n t -> p g (n t)").bitcast(I32),
         }
         h_sb = c_sb[:, I_DIM:K_DIM]
+        COL_TAU, COL_MOD, COL_TGT, COL_BIAS, ROW_DT = 0, 16, 32, 48, 64
 
         def plane_of(w, g):
             first = 0 if w == "mod" else 2
             return (first + g // 4, 4 * (g % 4))
 
-        nc.vector.memset(ltr[:].bitcast(I32), 0)
-        nc.vector.memset(planes[:, 0:1, :].bitcast(I32), 0)
-        nc.vector.memset(rows[:].bitcast(I32), 0)
-        nc.vector.memset(planes[:, 1:2, :].bitcast(I32), 0)
+        nc.vector.memset(vec_rows[:].bitcast(I32), 0)
         nc.vector.memset(warm[:], 0.0)
-        nc.vector.memset(planes[:, 2:4, :].bitcast(I32), 0)
+        for s in range(4):
+            nc.vector.memset(planes[:, s : s + 1, :].bitcast(I32), 0)
         masks.make_identity(nc, ident_f[:])
         masks.make_identity(nc, ident_b[:])
 
-        def load_planes(queue, view, slot, src):
+        def load_planes(slot, src):
             n_rows = 4 * src.shape[0]
             for q in range(4):
-                queue.dma_start(
-                    out=planes[32 * q : 32 * q + n_rows, slot, :].bitcast(view),
-                    in_=src[:, 4 * q : 4 * q + 4, :].bitcast(view),
+                nc.gpsimd.dma_start(
+                    out=planes[32 * q : 32 * q + n_rows, slot, :].bitcast(F32),
+                    in_=src[:, 4 * q : 4 * q + 4, :].bitcast(F32),
                 )
 
-        def load_words(w, j, g0, g1):
-            cols = slice(CHUNK * j, CHUNK * (j + 1))
-            nc.sync.dma_start(out=words[w][:, g0:g1, cols], in_=src_words[w][:, g0:g1, cols])
-
-        order = (("mod", 0), ("mod", 1), ("mod", 2), ("mod", 3), ("tgt", 0), ("tgt", 1), ("tgt", 2), ("tgt", 3))
+        def load_words(w, n0, n1, g0, g1):
+            nc.sync.dma_start(out=words[w][:, g0:g1, n0:n1], in_=src_words[w][:, g0:g1, n0:n1])
 
         nc.sync.dma_start(out=c_sb[:, 0:I_DIM], in_=x)
         nc.sync.dma_start(out=c_sb[:, I_DIM:K_DIM], in_=h)
-        nc.scalar.dma_start(out=ltr[0:16, :], in_=log_tau.rearrange("(c j) -> c j", c=16))
-        nc.scalar.dma_start(out=ltr[16:17, :], in_=time_delta.rearrange("p o -> o p"))
-        load_planes(nc.sync, I32, 0, W_mod_scales[0:4])
-        nc.scalar.dma_start(out=rows[0:1, :], in_=b_mod.unsqueeze(0))
-        nc.scalar.dma_start(out=rows[64:65, :], in_=bias.unsqueeze(0))
-        load_words("mod", 0, 0, 3)
-        load_planes(nc.sync, I32, 1, W_mod_scales[4:6])
-        load_words("mod", 0, 3, 6)
-        nc.scalar.dma_start(out=rows[32:33, :], in_=b_tgt.unsqueeze(0))
+        for vec, first in ((log_tau, COL_TAU), (b_mod, COL_MOD), (b_tgt, COL_TGT), (bias, COL_BIAS)):
+            nc.scalar.dma_start(out=vec_rows[first : first + 16, :], in_=vec.rearrange("(c j) -> c j", c=16))
+        nc.scalar.dma_start(out=vec_rows[ROW_DT : ROW_DT + 1, :], in_=time_delta.rearrange("p o -> o p"))
         nc.scalar.activation(out=warm_out[:], in_=warm[:], func=ACT.Exp)
-        load_planes(nc.gpsimd, F32, 2, W_tgt_scales[0:4])
-        load_planes(nc.gpsimd, F32, 3, W_tgt_scales[4:6])
-        for w, j in order[1:]:
-            cuts = (0, 3, 5, 6) if (w, j) == order[-1] else (0, 3, 6)
+        load_planes(0, W_mod_scales[0:4])
+        load_planes(1, W_mod_scales[4:6])
+        load_planes(2, W_tgt_scales[0:4])
+        load_planes(3, W_tgt_scales[4:6])
+        for w, n0, n1, cuts in (
+            ("mod", 0, 1024, (0, 3, 6)),
+            ("mod", 1024, 2048, (0, 3, 6)),
+            ("tgt", 0, 1024, (0, 3, 6)),
+            ("tgt", 1024, 1536, (0, 3, 6)),
+            ("tgt", 1536, 2048, (0, 3, 5, 6)),
+        ):
             for i in range(len(cuts) - 1):
-                load_words(w, j, cuts[i], cuts[i + 1])
+                load_words(w, n0, n1, cuts[i], cuts[i + 1])
 
         c32 = c_sb[:].bitcast(F32)
         g32 = grouped[:].bitcast(F32).rearrange("p (g t u) -> p g t u", g=GROUPS, t=P, u=2)
         for b in range(3):
-            if b < 2:
-                xt = psm.tile([P, 2, 2, P], F32, tag="misc", name="xt%d" % b)
-            else:
-                xt = psab.tile([P, 2, 2, P], F32, tag="be", name="xt%d" % b)
+            xt = pst.tile([P, 2, 2, P], F32, tag="t", name="xt%d" % b)
             for gi in range(2):
                 g = 2 * b + gi
                 for u in range(2):
-                    nc.tensor.transpose(
-                        xt[:, gi, u, :], c32[:, 256 * g + u : 256 * (g + 1) : 2], ident_f[:]
-                    )
+                    nc.tensor.transpose(xt[:, gi, u, :], c32[:, 256 * g + u : 256 * (g + 1) : 2], ident_f[:])
             src = xt[:].rearrange("p g u t -> p g t u")
             if b == 1:
                 nc.scalar.copy(out=g32[:, 2 * b : 2 * b + 2], in_=src)
@@ -151,161 +143,192 @@ def tile_ltccell_w_kernel(
             in_=grouped[:, 1024:3072],
         )
 
-        ps_lt = psab.tile([P, P], BF16, tag="al", name="ps_lt")
-        nc.tensor.transpose(ps_lt[:], ltr[:], ident_b[:])
-        nc.scalar.activation(out=tau[:], in_=ps_lt[:, 0:16], func=ACT.Exp)
-        nc.vector.tensor_scalar(
-            out=ndt[:], in0=ps_lt[:, 16:17], scalar1=-1.0, scalar2=None, op0=ALU.mult
+        ps_vec = pst.tile([P, P], BF16, tag="t", name="ps_vec")
+        nc.tensor.transpose(ps_vec[:], vec_rows[:], ident_b[:])
+        ps_dt = pst.tile([P, P], F32, tag="t", name="ps_dt")
+        nc.tensor.matmul(
+            ps_dt[:],
+            lhsT=ident_b[:, ROW_DT : ROW_DT + 1].to_broadcast([P, P]),
+            rhs=vec_rows[:],
+            start=True,
+            stop=True,
         )
-        nc.vector.tensor_scalar(out=tau_eps[:], in0=tau[:], scalar1=EPS, scalar2=None, op0=ALU.add)
-        nc.vector.reciprocal(out=alpha[:], in_=tau_eps[:])
+        nc.vector.tensor_copy(out=vec_cols[:], in_=ps_vec[:, 0:64])
+        nc.vector.tensor_copy(out=dt_all[:], in_=ps_dt[:])
+        nc.scalar.activation(out=r_tau[:], in_=vec_cols[:, COL_TAU : COL_TAU + 16], func=ACT.Exp, scale=-1.0)
         nc.vector.tensor_scalar(
-            out=beta[:], in0=alpha[:], scalar1=-EPS, scalar2=1.0, op0=ALU.mult, op1=ALU.add
+            out=damp[:], in0=r_tau[:], scalar1=EPS, scalar2=1.0, op0=ALU.mult, op1=ALU.add
+        )
+        nc.vector.scalar_tensor_tensor(
+            out=shift[:], in0=r_tau[:], scalar=INV_EPS, in1=r_tau[:], op0=ALU.add, op1=ALU.mult
+        )
+        nc.vector.reciprocal(out=damp[:], in_=damp[:])
+        nc.vector.scalar_tensor_tensor(
+            out=rate[:], in0=damp[:], scalar=EPS, in1=damp[:], op0=ALU.mult, op1=ALU.mult
         )
 
-        def spread_row(row, half, name):
-            ps = psm.tile([P, 1024], BF16, tag="misc", name=name)
-            for i in range(2):
-                n0 = 1024 * half + 512 * i
-                nc.tensor.matmul(
-                    ps[:, 512 * i : 512 * (i + 1)],
-                    lhsT=ident_b[:, row : row + 1].to_broadcast([P, P]),
-                    rhs=rows[:, n0 : n0 + 512],
-                    start=True,
-                    stop=True,
-                )
-            return ps
-
-        def spread_small(small, j, tag):
-            ps = psab.tile([P, CHUNK], F32, tag=tag, name="%s%d" % (tag, j))
-            for i in range(4):
-                c = 4 * j + i
-                nc.tensor.transpose(
-                    ps[:, P * i : P * (i + 1)], small[:, c : c + 1].to_broadcast([P, P]), ident_f[:]
-                )
-            return ps
-
-        def prep_bmod(half):
-            ps = spread_row(0, half, "ps_bmod%d" % half)
-            nc.scalar.copy(out=bmod_b[:, 1024 * half : 1024 * (half + 1)], in_=ps[:])
-
-        def prep_btgt(half):
-            ps = spread_row(32, half, "ps_btgt%d" % half)
-            nc.scalar.copy(out=btgt_b[:, 1024 * half : 1024 * (half + 1)], in_=ps[:])
-
-        def prep_hb(half):
-            cols = slice(1024 * half, 1024 * (half + 1))
-            ps = spread_row(64, half, "ps_bias%d" % half)
-            nc.vector.tensor_tensor(out=hb[:, cols], in0=h_sb[:, cols], in1=ps[:], op=ALU.subtract)
-
-        def cols_of(j):
-            return slice(CHUNK * j, CHUNK * (j + 1))
-
-        def mx_passes(w, j):
-            acc = psz.tile([P, CHUNK], F32, tag="z" + w, name="z_%s%d" % (w, j))
-            for g in range(GROUPS):
+        def passes(w, blk, acc, g0, g1):
+            cols = slice(P * blk, P * (blk + 1))
+            for g in range(g0, g1):
                 slot, k = plane_of(w, g)
                 nc.tensor.matmul_mx(
-                    out=acc[:],
-                    lhsT=c_codes[:, P * g : P * (g + 1)].bitcast(FP8X4),
-                    lhsT_scale=c_scales[:, P * g : P * (g + 1)],
-                    rhs=words[w][:, g, cols_of(j)].bitcast(FP8X4),
-                    rhs_scale=planes[k:P, slot, cols_of(j)],
+                    out=acc,
+                    lhsT=words[w][:, g, cols].bitcast(FP8X4),
+                    lhsT_scale=planes[k:P, slot, cols],
+                    rhs=c_codes[:, P * g : P * (g + 1)].bitcast(FP8X4),
+                    rhs_scale=c_scales[:, P * g : P * (g + 1)],
                     start=(g == 0),
                     stop=(g == GROUPS - 1),
                 )
-            return acc
 
         live = {}
 
-        def pieces_of(w, j):
-            n = 2 if (w, j) == order[-1] else 1
-            width = CHUNK // n
-            return [(width * i, width * (i + 1)) for i in range(n)]
+        def mx(w, j):
+            z = psz.tile([P, PER_CHUNK, P], F32, tag="z", name="z_%s%d" % (w, j))
+            for i in range(PER_CHUNK):
+                passes(w, PER_CHUNK * j + i, z[:, i, :], 0, GROUPS)
+            live[(w, j)] = [z[:, i, :] for i in range(PER_CHUNK)]
 
-        def bias_add(w, j, acc):
-            b_b = bmod_b if w == "mod" else btgt_b
-            z_t = work.tile([P, CHUNK], F32, tag="s" + w, name="s_%s%d" % (w, j))
-            live[(w, j)] = z_t
-            for lo, hi in pieces_of(w, j):
-                nc.vector.tensor_tensor(
-                    out=z_t[:, lo:hi],
-                    in0=acc[:, lo:hi],
-                    in1=b_b[:, CHUNK * j + lo : CHUNK * j + hi],
-                    op=ALU.add,
+        def block_cols(j, i):
+            return slice(CHUNK * j + P * i, CHUNK * j + P * (i + 1))
+
+        def mod_tanh(j):
+            g_t = work.tile([P, CHUNK], F32, tag="g", name="g%d" % j)
+            live[("g", j)] = g_t
+            for i in range(PER_CHUNK):
+                c = COL_MOD + PER_CHUNK * j + i
+                nc.scalar.activation(
+                    out=g_t[:, P * i : P * (i + 1)],
+                    in_=live[("mod", j)][i],
+                    func=ACT.Abs,
+                    bias=vec_cols[:, c : c + 1],
                 )
-            for lo, hi in pieces_of(w, j):
-                if w == "mod":
-                    nc.scalar.activation(out=z_t[:, lo:hi], in_=z_t[:, lo:hi], func=ACT.Abs)
-                nc.scalar.activation(out=z_t[:, lo:hi], in_=z_t[:, lo:hi], func=ACT.Tanh)
+            nc.scalar.activation(out=g_t[:], in_=g_t[:], func=ACT.Tanh)
 
-        def mod_a(j):
-            a1_t = work.tile([P, CHUNK], F32, tag="a1", name="a1_%d" % j)
-            q_t = work.tile([P, CHUNK], F32, tag="q", name="q%d" % j)
-            live[("a1", j)] = a1_t
-            live[("q", j)] = q_t
-            nc.vector.tensor_tensor(out=a1_t[:], in0=live[("mod", j)][:], in1=live[("be", j)][:], op=ALU.mult)
-            nc.scalar.activation(out=q_t[:], in_=a1_t[:], func=ACT.Copy, bias=1.0, scale=-EPS)
-
-        def mod_b(j):
-            r_t = work.tile([P, CHUNK], F32, tag="r", name="r%d" % j)
-            live[("r", j)] = r_t
-            nc.vector.tensor_tensor(out=r_t[:], in0=live[("a1", j)][:], in1=live[("al", j)][:], op=ALU.add)
-
-        def mod_c(j):
-            cols = cols_of(j)
-            r_t = live[("r", j)]
-            nc.vector.tensor_tensor(out=r_t[:], in0=r_t[:], in1=live[("q", j)][:], op=ALU.mult)
-            nc.scalar.activation(out=r_t[:], in_=r_t[:], func=ACT.Exp, scale=ndt[:, 0:1])
-            nc.scalar.activation(out=q_all[:, cols], in_=r_t[:], func=ACT.Copy, bias=1.0, scale=-1.0)
-            nc.gpsimd.tensor_tensor(out=p_all[:, cols], in0=q_all[:, cols], in1=hb[:, cols], op=ALU.mult)
-            nc.gpsimd.tensor_tensor(out=p_all[:, cols], in0=h_sb[:, cols], in1=p_all[:, cols], op=ALU.subtract)
-
-        def tgt_a(j):
-            a_t = live[("tgt", j)]
-            for lo, hi in pieces_of("tgt", j):
-                nc.vector.tensor_tensor(
-                    out=a_t[:, lo:hi],
-                    in0=a_t[:, lo:hi],
-                    in1=q_all[:, CHUNK * j + lo : CHUNK * j + hi],
-                    op=ALU.mult,
+        def mod_rate(j):
+            g_t = live[("g", j)]
+            w_t = work.tile([P, CHUNK], F32, tag="w", name="w%d" % j)
+            v_t = work.tile([P, CHUNK], F32, tag="v", name="v%d" % j)
+            live[("v", j)] = v_t
+            nc.vector.scalar_tensor_tensor(
+                out=w_t[:], in0=g_t[:], scalar=-INV_EPS, in1=g_t[:], op0=ALU.add, op1=ALU.mult
+            )
+            for i in range(PER_CHUNK):
+                c = PER_CHUNK * j + i
+                nc.vector.scalar_tensor_tensor(
+                    out=v_t[:, P * i : P * (i + 1)],
+                    in0=w_t[:, P * i : P * (i + 1)],
+                    scalar=shift[:, c : c + 1],
+                    in1=dt_all[:],
+                    op0=ALU.subtract,
+                    op1=ALU.mult,
                 )
 
-        def tgt_b(j):
+        def mod_exp(j):
+            v_t = live[("v", j)]
+            for i in range(PER_CHUNK):
+                c = PER_CHUNK * j + i
+                nc.scalar.activation(
+                    out=v_t[:, P * i : P * (i + 1)],
+                    in_=v_t[:, P * i : P * (i + 1)],
+                    func=ACT.Exp,
+                    scale=rate[:, c : c + 1],
+                )
+
+        def mod_turn(j):
+            v_t = live[("v", j)]
+            ps = pst.tile([P, CHUNK], F32, tag="t", name="ps_d%d" % j)
+            for i in range(PER_CHUNK):
+                nc.tensor.transpose(ps[:, P * i : P * (i + 1)], v_t[:, P * i : P * (i + 1)], ident_f[:])
+            cols = slice(CHUNK * j, CHUNK * (j + 1))
+            nc.vector.tensor_scalar(
+                out=q_all[:, cols], in0=v_t[:], scalar1=-1.0, scalar2=1.0, op0=ALU.mult, op1=ALU.add
+            )
+            nc.vector.tensor_tensor(out=dh_all[:, cols], in0=ps[:], in1=h_sb[:, cols], op=ALU.mult)
+
+        def tgt_tanh(j):
+            a_t = work.tile([P, CHUNK], F32, tag="a", name="a%d" % j)
+            live[("a", j)] = a_t
+            for i in range(PER_CHUNK):
+                c = COL_TGT + PER_CHUNK * j + i
+                nc.scalar.activation(
+                    out=a_t[:, P * i : P * (i + 1)],
+                    in_=live[("tgt", j)][i],
+                    func=ACT.Tanh,
+                    bias=vec_cols[:, c : c + 1],
+                )
+
+        def tgt_mix(j):
+            a_t = live[("a", j)]
+            for i in range(PER_CHUNK):
+                c = COL_BIAS + PER_CHUNK * j + i
+                nc.vector.scalar_tensor_tensor(
+                    out=a_t[:, P * i : P * (i + 1)],
+                    in0=a_t[:, P * i : P * (i + 1)],
+                    scalar=vec_cols[:, c : c + 1],
+                    in1=q_all[:, block_cols(j, i)],
+                    op0=ALU.add,
+                    op1=ALU.mult,
+                )
+
+        def tgt_turn(j, pieces):
+            a_t = live[("a", j)]
             o_t = work.tile([P, CHUNK], F32, tag="o", name="o%d" % j)
-            for lo, hi in pieces_of("tgt", j):
-                cols = slice(CHUNK * j + lo, CHUNK * j + hi)
+            n = PER_CHUNK // pieces
+            width = n * P
+            turned = []
+            for s in range(pieces):
+                ps = pst.tile([P, width], F32, tag="t", name="ps_u%d_%d" % (j, s))
+                turned.append(ps)
+                for i in range(n):
+                    b = n * s + i
+                    nc.tensor.transpose(ps[:, P * i : P * (i + 1)], a_t[:, P * b : P * (b + 1)], ident_f[:])
+            for s in range(pieces):
+                cols = slice(CHUNK * j + width * s, CHUNK * j + width * (s + 1))
+                o_cols = slice(width * s, width * (s + 1))
                 nc.vector.tensor_tensor(
-                    out=o_t[:, lo:hi], in0=live[("tgt", j)][:, lo:hi], in1=p_all[:, cols], op=ALU.add
+                    out=o_t[:, o_cols], in0=turned[s][:], in1=dh_all[:, cols], op=ALU.add
                 )
-                nc.sync.dma_start(out=out[:, cols], in_=o_t[:, lo:hi])
+                nc.sync.dma_start(out=out[:, cols], in_=o_t[:, o_cols])
 
-        prep_bmod(0)
-        prep_hb(0)
-        prep_bmod(1)
-        prep_hb(1)
-        preps = {1: 0, 2: 1}
-        n_events = len(order)
-        for k in range(n_events + 2):
-            acc = None
-            if k < n_events:
-                acc = mx_passes(order[k][0], order[k][1])
-            if 2 <= k and order[k - 2][0] == "mod":
-                mod_c(order[k - 2][1])
-            if 1 <= k <= n_events:
-                if order[k - 1][0] == "mod":
-                    mod_a(order[k - 1][1])
-                else:
-                    tgt_a(order[k - 1][1])
-            if k < n_events:
-                bias_add(order[k][0], order[k][1], acc)
-            if 1 <= k <= n_events:
-                if order[k - 1][0] == "mod":
-                    mod_b(order[k - 1][1])
-                else:
-                    tgt_b(order[k - 1][1])
-            if k < n_events and order[k][0] == "mod":
-                live[("be", order[k][1])] = spread_small(beta, order[k][1], "be")
-                live[("al", order[k][1])] = spread_small(alpha, order[k][1], "al")
-            if k in preps:
-                prep_btgt(preps[k])
+        mx("mod", 0)
+        mod_tanh(0)
+        mod_rate(0)
+        mx("mod", 1)
+        mod_tanh(1)
+        mod_exp(0)
+        mod_rate(1)
+        mod_turn(0)
+        mod_exp(1)
+        mod_turn(1)
+        mx("mod", 2)
+        mod_tanh(2)
+        mod_rate(2)
+        mx("mod", 3)
+        mod_tanh(3)
+        mod_exp(2)
+        mod_rate(3)
+        mod_turn(2)
+        mod_exp(3)
+        mx("tgt", 0)
+        mod_turn(3)
+        tgt_tanh(0)
+        tgt_mix(0)
+        mx("tgt", 1)
+        tgt_tanh(1)
+        tgt_turn(0, 1)
+        tgt_mix(1)
+        mx("tgt", 2)
+        tgt_tanh(2)
+        tgt_turn(1, 1)
+        tgt_mix(2)
+        last = [psz.tile([P, P], F32, tag="z", name="z_last%d" % i) for i in range(PER_CHUNK)]
+        live[("tgt", 3)] = [t[:] for t in last]
+        for i in range(PER_CHUNK):
+            passes("tgt", 12 + i, last[i][:], 0, GROUPS - 1)
+        tgt_turn(2, 1)
+        for i in range(PER_CHUNK):
+            passes("tgt", 12 + i, last[i][:], GROUPS - 1, GROUPS)
+        tgt_tanh(3)
+        tgt_mix(3)
+        tgt_turn(3, 2)

@@ -93,9 +93,9 @@ def tile_ltccell_w_kernel(
         def load_planes(slot, src):
             n_rows = 4 * src.shape[0]
             for q in range(4):
-                nc.gpsimd.dma_start(
-                    out=planes[32 * q : 32 * q + n_rows, slot, :].bitcast(F32),
-                    in_=src[:, 4 * q : 4 * q + 4, :].bitcast(F32),
+                nc.sync.dma_start(
+                    out=planes[32 * q : 32 * q + n_rows, slot, :].bitcast(I32),
+                    in_=src[:, 4 * q : 4 * q + 4, :].bitcast(I32),
                 )
 
         def load_words(w, n0, n1, g0, g1):
@@ -107,19 +107,17 @@ def tile_ltccell_w_kernel(
             nc.scalar.dma_start(out=vec_rows[first : first + 16, :], in_=vec.rearrange("(c j) -> c j", c=16))
         nc.scalar.dma_start(out=vec_rows[ROW_DT : ROW_DT + 1, :], in_=time_delta.rearrange("p o -> o p"))
         nc.scalar.activation(out=warm_out[:], in_=warm[:], func=ACT.Exp)
+        load_words("mod", 0, 1024, 0, 3)
         load_planes(0, W_mod_scales[0:4])
+        load_words("mod", 0, 1024, 3, 6)
         load_planes(1, W_mod_scales[4:6])
+        load_words("mod", 1024, 2048, 0, 3)
         load_planes(2, W_tgt_scales[0:4])
+        load_words("mod", 1024, 2048, 3, 6)
         load_planes(3, W_tgt_scales[4:6])
-        for w, n0, n1, cuts in (
-            ("mod", 0, 1024, (0, 3, 6)),
-            ("mod", 1024, 2048, (0, 3, 6)),
-            ("tgt", 0, 1024, (0, 3, 6)),
-            ("tgt", 1024, 1536, (0, 3, 6)),
-            ("tgt", 1536, 2048, (0, 3, 5, 6)),
-        ):
+        for n0, n1, cuts in ((0, 512, (0, 3, 6)), (512, 1024, (0, 3, 6)), (1024, 1536, (0, 3, 6)), (1536, 2048, (0, 3, 5, 6))):
             for i in range(len(cuts) - 1):
-                load_words(w, n0, n1, cuts[i], cuts[i + 1])
+                load_words("tgt", n0, n1, cuts[i], cuts[i + 1])
 
         c32 = c_sb[:].bitcast(F32)
         g32 = grouped[:].bitcast(F32).rearrange("p (g t u) -> p g t u", g=GROUPS, t=P, u=2)
@@ -235,15 +233,22 @@ def tile_ltccell_w_kernel(
                     scale=rate[:, c : c + 1],
                 )
 
+        def mod_rest(j):
+            nc.vector.tensor_scalar(
+                out=q_all[:, CHUNK * j : CHUNK * (j + 1)],
+                in0=live[("v", j)][:],
+                scalar1=-1.0,
+                scalar2=1.0,
+                op0=ALU.mult,
+                op1=ALU.add,
+            )
+
         def mod_turn(j):
             v_t = live[("v", j)]
             ps = pst.tile([P, CHUNK], F32, tag="t", name="ps_d%d" % j)
             for i in range(PER_CHUNK):
                 nc.tensor.transpose(ps[:, P * i : P * (i + 1)], v_t[:, P * i : P * (i + 1)], ident_f[:])
             cols = slice(CHUNK * j, CHUNK * (j + 1))
-            nc.vector.tensor_scalar(
-                out=q_all[:, cols], in0=v_t[:], scalar1=-1.0, scalar2=1.0, op0=ALU.mult, op1=ALU.add
-            )
             nc.vector.tensor_tensor(out=dh_all[:, cols], in0=ps[:], in1=h_sb[:, cols], op=ALU.mult)
 
         def tgt_tanh(j):
@@ -298,30 +303,34 @@ def tile_ltccell_w_kernel(
         mod_tanh(1)
         mod_exp(0)
         mod_rate(1)
-        mod_turn(0)
-        mod_exp(1)
-        mod_turn(1)
+        mod_rest(0)
         mx("mod", 2)
         mod_tanh(2)
+        mod_exp(1)
         mod_rate(2)
+        mod_turn(0)
+        mod_rest(1)
         mx("mod", 3)
         mod_tanh(3)
         mod_exp(2)
         mod_rate(3)
-        mod_turn(2)
-        mod_exp(3)
+        mod_turn(1)
+        mod_rest(2)
         mx("tgt", 0)
-        mod_turn(3)
         tgt_tanh(0)
+        mod_exp(3)
         tgt_mix(0)
+        mod_turn(2)
+        mod_rest(3)
         mx("tgt", 1)
         tgt_tanh(1)
-        tgt_turn(0, 1)
         tgt_mix(1)
+        mod_turn(3)
+        tgt_turn(0, 1)
         mx("tgt", 2)
         tgt_tanh(2)
-        tgt_turn(1, 1)
         tgt_mix(2)
+        tgt_turn(1, 1)
         last = [psz.tile([P, P], F32, tag="z", name="z_last%d" % i) for i in range(PER_CHUNK)]
         live[("tgt", 3)] = [t[:] for t in last]
         for i in range(PER_CHUNK):

@@ -107,17 +107,21 @@ def tile_ltccell_w_kernel(
             nc.scalar.dma_start(out=vec_rows[first : first + 16, :], in_=vec.rearrange("(c j) -> c j", c=16))
         nc.scalar.dma_start(out=vec_rows[ROW_DT : ROW_DT + 1, :], in_=time_delta.rearrange("p o -> o p"))
         nc.scalar.activation(out=warm_out[:], in_=warm[:], func=ACT.Exp)
-        load_words("mod", 0, 1024, 0, 3)
         load_planes(0, W_mod_scales[0:4])
-        load_words("mod", 0, 1024, 3, 6)
+        load_words("mod", 0, 512, 0, 3)
         load_planes(1, W_mod_scales[4:6])
-        load_words("mod", 1024, 2048, 0, 3)
-        load_planes(2, W_tgt_scales[0:4])
-        load_words("mod", 1024, 2048, 3, 6)
-        load_planes(3, W_tgt_scales[4:6])
-        for n0, n1, cuts in ((0, 512, (0, 3, 6)), (512, 1024, (0, 3, 6)), (1024, 1536, (0, 3, 6)), (1536, 2048, (0, 3, 5, 6))):
+        load_words("mod", 0, 512, 3, 6)
+        for j in range(1, CHUNKS):
+            load_words("mod", CHUNK * j, CHUNK * (j + 1), 0, 3)
+            if j == 2:
+                load_planes(2, W_tgt_scales[0:4])
+            if j == 3:
+                load_planes(3, W_tgt_scales[4:6])
+            load_words("mod", CHUNK * j, CHUNK * (j + 1), 3, 6)
+        for j in range(CHUNKS):
+            cuts = (0, 3, 6) if j < CHUNKS - 1 else (0, 3, 5, 6)
             for i in range(len(cuts) - 1):
-                load_words("tgt", n0, n1, cuts[i], cuts[i + 1])
+                load_words("tgt", CHUNK * j, CHUNK * (j + 1), cuts[i], cuts[i + 1])
 
         c32 = c_sb[:].bitcast(F32)
         g32 = grouped[:].bitcast(F32).rearrange("p (g t u) -> p g t u", g=GROUPS, t=P, u=2)

@@ -90,12 +90,12 @@ def tile_ltccell_w_kernel(
         masks.make_identity(nc, ident_f[:])
         masks.make_identity(nc, ident_b[:])
 
-        def load_planes(slot, src):
+        def load_planes(queue, view, slot, src):
             n_rows = 4 * src.shape[0]
             for q in range(4):
-                nc.sync.dma_start(
-                    out=planes[32 * q : 32 * q + n_rows, slot, :].bitcast(I32),
-                    in_=src[:, 4 * q : 4 * q + 4, :].bitcast(I32),
+                queue.dma_start(
+                    out=planes[32 * q : 32 * q + n_rows, slot, :].bitcast(view),
+                    in_=src[:, 4 * q : 4 * q + 4, :].bitcast(view),
                 )
 
         def load_words(w, n0, n1, g0, g1):
@@ -107,21 +107,19 @@ def tile_ltccell_w_kernel(
             nc.scalar.dma_start(out=vec_rows[first : first + 16, :], in_=vec.rearrange("(c j) -> c j", c=16))
         nc.scalar.dma_start(out=vec_rows[ROW_DT : ROW_DT + 1, :], in_=time_delta.rearrange("p o -> o p"))
         nc.scalar.activation(out=warm_out[:], in_=warm[:], func=ACT.Exp)
-        load_planes(0, W_mod_scales[0:4])
-        load_words("mod", 0, 512, 0, 3)
-        load_planes(1, W_mod_scales[4:6])
-        load_words("mod", 0, 512, 3, 6)
-        for j in range(1, CHUNKS):
-            load_words("mod", CHUNK * j, CHUNK * (j + 1), 0, 3)
-            if j == 2:
-                load_planes(2, W_tgt_scales[0:4])
-            if j == 3:
-                load_planes(3, W_tgt_scales[4:6])
-            load_words("mod", CHUNK * j, CHUNK * (j + 1), 3, 6)
-        for j in range(CHUNKS):
-            cuts = (0, 3, 6) if j < CHUNKS - 1 else (0, 3, 5, 6)
+        load_planes(nc.sync, I32, 0, W_mod_scales[0:4])
+        load_planes(nc.sync, I32, 1, W_mod_scales[4:6])
+        load_planes(nc.gpsimd, F32, 2, W_tgt_scales[0:4])
+        load_planes(nc.gpsimd, F32, 3, W_tgt_scales[4:6])
+        for w, n0, n1, cuts in (
+            ("mod", 0, 1024, (0, 3, 6)),
+            ("mod", 1024, 2048, (0, 3, 6)),
+            ("tgt", 0, 1024, (0, 3, 6)),
+            ("tgt", 1024, 1536, (0, 3, 6)),
+            ("tgt", 1536, 2048, (0, 3, 5, 6)),
+        ):
             for i in range(len(cuts) - 1):
-                load_words("tgt", CHUNK * j, CHUNK * (j + 1), cuts[i], cuts[i + 1])
+                load_words(w, n0, n1, cuts[i], cuts[i + 1])
 
         c32 = c_sb[:].bitcast(F32)
         g32 = grouped[:].bitcast(F32).rearrange("p (g t u) -> p g t u", g=GROUPS, t=P, u=2)
@@ -308,28 +306,28 @@ def tile_ltccell_w_kernel(
         mod_exp(0)
         mod_rate(1)
         mod_rest(0)
+        mod_exp(1)
+        mod_rest(1)
         mx("mod", 2)
         mod_tanh(2)
-        mod_exp(1)
-        mod_rate(2)
         mod_turn(0)
-        mod_rest(1)
+        mod_rate(2)
         mx("mod", 3)
         mod_tanh(3)
         mod_exp(2)
-        mod_rate(3)
         mod_turn(1)
+        mod_rate(3)
         mod_rest(2)
         mx("tgt", 0)
-        tgt_tanh(0)
         mod_exp(3)
-        tgt_mix(0)
+        tgt_tanh(0)
         mod_turn(2)
         mod_rest(3)
+        tgt_mix(0)
         mx("tgt", 1)
         tgt_tanh(1)
-        tgt_mix(1)
         mod_turn(3)
+        tgt_mix(1)
         tgt_turn(0, 1)
         mx("tgt", 2)
         tgt_tanh(2)
@@ -338,10 +336,12 @@ def tile_ltccell_w_kernel(
         last = [psz.tile([P, P], F32, tag="z", name="z_last%d" % i) for i in range(PER_CHUNK)]
         live[("tgt", 3)] = [t[:] for t in last]
         for i in range(PER_CHUNK):
-            passes("tgt", 12 + i, last[i][:], 0, GROUPS - 1)
+            passes("tgt", 12 + i, last[i][:], 0, 3)
         tgt_turn(2, 1)
         for i in range(PER_CHUNK):
-            passes("tgt", 12 + i, last[i][:], GROUPS - 1, GROUPS)
+            passes("tgt", 12 + i, last[i][:], 3, 5)
+        for i in range(PER_CHUNK):
+            passes("tgt", 12 + i, last[i][:], 5, 6)
         tgt_tanh(3)
         tgt_mix(3)
         tgt_turn(3, 2)

@@ -80,8 +80,9 @@ def tile_ltccell_w_kernel(
         COL_TAU, COL_MOD, COL_TGT, COL_BIAS, ROW_DT = 0, 16, 32, 48, 64
 
         def plane_of(w, g):
-            first = 0 if w == "mod" else 2
-            return (first + g // 4, 4 * (g % 4))
+            if w == "mod":
+                return (g // 4, 4 * (g % 4))
+            return (2, 4 * g) if g < 4 else (3, 4 * (g - 2))
 
         nc.vector.memset(vec_rows[:].bitcast(I32), 0)
         nc.vector.memset(warm[:], 0.0)
@@ -90,12 +91,12 @@ def tile_ltccell_w_kernel(
         masks.make_identity(nc, ident_f[:])
         masks.make_identity(nc, ident_b[:])
 
-        def load_planes(queue, view, slot, src):
+        def load_planes(slot, k, src):
             n_rows = 4 * src.shape[0]
             for q in range(4):
-                queue.dma_start(
-                    out=planes[32 * q : 32 * q + n_rows, slot, :].bitcast(view),
-                    in_=src[:, 4 * q : 4 * q + 4, :].bitcast(view),
+                nc.sync.dma_start(
+                    out=planes[32 * q + k : 32 * q + k + n_rows, slot, :].bitcast(I32),
+                    in_=src[:, 4 * q : 4 * q + 4, :].bitcast(I32),
                 )
 
         def load_words(w, n0, n1, g0, g1):
@@ -103,18 +104,19 @@ def tile_ltccell_w_kernel(
 
         nc.sync.dma_start(out=c_sb[:, 0:I_DIM], in_=x)
         nc.sync.dma_start(out=c_sb[:, I_DIM:K_DIM], in_=h)
+        nc.scalar.activation(out=warm_out[:], in_=warm[:], func=ACT.Exp)
+        load_planes(0, 0, W_mod_scales[0:4])
+        load_planes(1, 0, W_mod_scales[4:6])
+        load_planes(2, 0, W_tgt_scales[0:4])
+        load_planes(3, 8, W_tgt_scales[4:6])
         for vec, first in ((log_tau, COL_TAU), (b_mod, COL_MOD), (b_tgt, COL_TGT), (bias, COL_BIAS)):
             nc.scalar.dma_start(out=vec_rows[first : first + 16, :], in_=vec.rearrange("(c j) -> c j", c=16))
         nc.scalar.dma_start(out=vec_rows[ROW_DT : ROW_DT + 1, :], in_=time_delta.rearrange("p o -> o p"))
-        nc.scalar.activation(out=warm_out[:], in_=warm[:], func=ACT.Exp)
-        load_planes(nc.sync, I32, 0, W_mod_scales[0:4])
-        load_planes(nc.sync, I32, 1, W_mod_scales[4:6])
-        load_planes(nc.gpsimd, F32, 2, W_tgt_scales[0:4])
-        load_planes(nc.gpsimd, F32, 3, W_tgt_scales[4:6])
         for w, n0, n1, cuts in (
             ("mod", 0, 1024, (0, 3, 6)),
             ("mod", 1024, 2048, (0, 3, 6)),
-            ("tgt", 0, 1024, (0, 3, 6)),
+            ("tgt", 0, 512, (0, 3, 6)),
+            ("tgt", 512, 1024, (0, 3, 6)),
             ("tgt", 1024, 1536, (0, 3, 6)),
             ("tgt", 1536, 2048, (0, 3, 5, 6)),
         ):

@@ -84,16 +84,16 @@ def tile_ltccell_w_kernel(
                 return (g // 4, 4 * (g % 4))
             return (2, 4 * g) if g < 4 else (3, 4 * (g - 2))
 
-        nc.vector.memset(vec_rows[:].bitcast(I32), 0)
         nc.vector.memset(warm[:], 0.0)
         for s in range(4):
             nc.vector.memset(planes[:, s : s + 1, :].bitcast(I32), 0)
+        nc.vector.memset(vec_rows[:].bitcast(I32), 0)
         masks.make_identity(nc, ident_f[:])
         masks.make_identity(nc, ident_b[:])
 
-        def load_planes(slot, k, src):
+        def load_planes(slot, k, src, quadrants):
             n_rows = 4 * src.shape[0]
-            for q in range(4):
+            for q in quadrants:
                 nc.sync.dma_start(
                     out=planes[32 * q + k : 32 * q + k + n_rows, slot, :].bitcast(I32),
                     in_=src[:, 4 * q : 4 * q + 4, :].bitcast(I32),
@@ -102,23 +102,27 @@ def tile_ltccell_w_kernel(
         def load_words(w, n0, n1, g0, g1):
             nc.sync.dma_start(out=words[w][:, g0:g1, n0:n1], in_=src_words[w][:, g0:g1, n0:n1])
 
+        nc.scalar.activation(out=warm_out[:], in_=warm[:], func=ACT.Exp)
+        load_planes(0, 0, W_mod_scales[0:4], (0, 1, 2, 3))
+        load_planes(1, 0, W_mod_scales[4:6], (0, 1))
         nc.sync.dma_start(out=c_sb[:, 0:I_DIM], in_=x)
         nc.sync.dma_start(out=c_sb[:, I_DIM:K_DIM], in_=h)
-        nc.scalar.activation(out=warm_out[:], in_=warm[:], func=ACT.Exp)
-        load_planes(0, 0, W_mod_scales[0:4])
-        load_planes(1, 0, W_mod_scales[4:6])
-        load_planes(2, 0, W_tgt_scales[0:4])
-        load_planes(3, 8, W_tgt_scales[4:6])
+        load_planes(1, 0, W_mod_scales[4:6], (2, 3))
+        load_planes(2, 0, W_tgt_scales[0:4], (0, 1, 2, 3))
+        load_planes(3, 8, W_tgt_scales[4:6], (0, 1, 2, 3))
+        load_words("mod", 0, 1024, 0, 3)
         for vec, first in ((log_tau, COL_TAU), (b_mod, COL_MOD), (b_tgt, COL_TGT), (bias, COL_BIAS)):
             nc.scalar.dma_start(out=vec_rows[first : first + 16, :], in_=vec.rearrange("(c j) -> c j", c=16))
         nc.scalar.dma_start(out=vec_rows[ROW_DT : ROW_DT + 1, :], in_=time_delta.rearrange("p o -> o p"))
         for w, n0, n1, cuts in (
-            ("mod", 0, 1024, (0, 3, 6)),
+            ("mod", 0, 1024, (3, 6)),
             ("mod", 1024, 2048, (0, 3, 6)),
             ("tgt", 0, 512, (0, 3, 6)),
             ("tgt", 512, 1024, (0, 3, 6)),
             ("tgt", 1024, 1536, (0, 3, 6)),
-            ("tgt", 1536, 2048, (0, 3, 5, 6)),
+            ("tgt", 1536, 2048, (0, 3)),
+            ("tgt", 1536, 1792, (3, 6)),
+            ("tgt", 1792, 2048, (3, 6)),
         ):
             for i in range(len(cuts) - 1):
                 load_words(w, n0, n1, cuts[i], cuts[i + 1])
@@ -341,9 +345,7 @@ def tile_ltccell_w_kernel(
             passes("tgt", 12 + i, last[i][:], 0, 3)
         tgt_turn(2, 1)
         for i in range(PER_CHUNK):
-            passes("tgt", 12 + i, last[i][:], 3, 5)
-        for i in range(PER_CHUNK):
-            passes("tgt", 12 + i, last[i][:], 5, 6)
+            passes("tgt", 12 + i, last[i][:], 3, GROUPS)
         tgt_tanh(3)
         tgt_mix(3)
         tgt_turn(3, 2)

@@ -85,35 +85,35 @@ def tile_ltccell_w_kernel(
             return (2, 4 * g) if g < 4 else (3, 4 * (g - 2))
 
         nc.vector.memset(warm[:], 0.0)
-        for s in range(4):
+        for s in (0, 1, 3, 2):
             nc.vector.memset(planes[:, s : s + 1, :].bitcast(I32), 0)
         nc.vector.memset(vec_rows[:].bitcast(I32), 0)
         masks.make_identity(nc, ident_f[:])
-        masks.make_identity(nc, ident_b[:])
 
-        def load_planes(slot, k, src, quadrants):
+        def load_planes(queue, view, slot, k, src, quadrants):
             n_rows = 4 * src.shape[0]
             for q in quadrants:
-                nc.sync.dma_start(
-                    out=planes[32 * q + k : 32 * q + k + n_rows, slot, :].bitcast(I32),
-                    in_=src[:, 4 * q : 4 * q + 4, :].bitcast(I32),
+                queue.dma_start(
+                    out=planes[32 * q + k : 32 * q + k + n_rows, slot, :].bitcast(view),
+                    in_=src[:, 4 * q : 4 * q + 4, :].bitcast(view),
                 )
 
         def load_words(w, n0, n1, g0, g1):
             nc.sync.dma_start(out=words[w][:, g0:g1, n0:n1], in_=src_words[w][:, g0:g1, n0:n1])
 
         nc.scalar.activation(out=warm_out[:], in_=warm[:], func=ACT.Exp)
-        load_planes(0, 0, W_mod_scales[0:4], (0, 1, 2, 3))
-        load_planes(1, 0, W_mod_scales[4:6], (0, 1))
+        load_planes(nc.sync, I32, 0, 0, W_mod_scales[0:4], (0, 1, 2, 3))
+        load_planes(nc.sync, I32, 1, 0, W_mod_scales[4:6], (0, 1))
         nc.sync.dma_start(out=c_sb[:, 0:I_DIM], in_=x)
         nc.sync.dma_start(out=c_sb[:, I_DIM:K_DIM], in_=h)
-        load_planes(1, 0, W_mod_scales[4:6], (2, 3))
-        load_planes(2, 0, W_tgt_scales[0:4], (0, 1, 2, 3))
-        load_planes(3, 8, W_tgt_scales[4:6], (0, 1, 2, 3))
+        load_planes(nc.sync, I32, 1, 0, W_mod_scales[4:6], (2, 3))
+        load_planes(nc.sync, I32, 2, 0, W_tgt_scales[0:4], (0, 1, 2, 3))
+        load_planes(nc.gpsimd, F32, 3, 8, W_tgt_scales[4:6], (0, 1, 2, 3))
+        masks.make_identity(nc, ident_b[:])
         load_words("mod", 0, 1024, 0, 3)
         for vec, first in ((log_tau, COL_TAU), (b_mod, COL_MOD), (b_tgt, COL_TGT), (bias, COL_BIAS)):
-            nc.scalar.dma_start(out=vec_rows[first : first + 16, :], in_=vec.rearrange("(c j) -> c j", c=16))
-        nc.scalar.dma_start(out=vec_rows[ROW_DT : ROW_DT + 1, :], in_=time_delta.rearrange("p o -> o p"))
+            nc.sync.dma_start(out=vec_rows[first : first + 16, :], in_=vec.rearrange("(c j) -> c j", c=16))
+        nc.sync.dma_start(out=vec_rows[ROW_DT : ROW_DT + 1, :], in_=time_delta.rearrange("p o -> o p"))
         for w, n0, n1, cuts in (
             ("mod", 0, 1024, (3, 6)),
             ("mod", 1024, 2048, (0, 3, 6)),
@@ -122,7 +122,7 @@ def tile_ltccell_w_kernel(
             ("tgt", 1024, 1536, (0, 3, 6)),
             ("tgt", 1536, 2048, (0, 3)),
             ("tgt", 1536, 1792, (3, 6)),
-            ("tgt", 1792, 2048, (3, 6)),
+            ("tgt", 1792, 2048, (3, 5, 6)),
         ):
             for i in range(len(cuts) - 1):
                 load_words(w, n0, n1, cuts[i], cuts[i + 1])
@@ -271,9 +271,9 @@ def tile_ltccell_w_kernel(
                     bias=vec_cols[:, c : c + 1],
                 )
 
-        def tgt_mix(j):
+        def tgt_mix(j, blocks=range(PER_CHUNK)):
             a_t = live[("a", j)]
-            for i in range(PER_CHUNK):
+            for i in blocks:
                 c = COL_BIAS + PER_CHUNK * j + i
                 nc.vector.scalar_tensor_tensor(
                     out=a_t[:, P * i : P * (i + 1)],
@@ -337,15 +337,17 @@ def tile_ltccell_w_kernel(
         tgt_turn(0, 1)
         mx("tgt", 2)
         tgt_tanh(2)
-        tgt_mix(2)
+        tgt_mix(2, (0, 1))
         tgt_turn(1, 1)
+        tgt_mix(2, (2, 3))
         last = [psz.tile([P, P], F32, tag="z", name="z_last%d" % i) for i in range(PER_CHUNK)]
         live[("tgt", 3)] = [t[:] for t in last]
-        for i in range(PER_CHUNK):
-            passes("tgt", 12 + i, last[i][:], 0, 3)
-        tgt_turn(2, 1)
-        for i in range(PER_CHUNK):
-            passes("tgt", 12 + i, last[i][:], 3, GROUPS)
+        for i, g0, g1 in (
+            (0, 0, 3), (1, 0, 3), (2, 0, 3), (3, 0, 3),
+            (0, 3, 6), (1, 3, 6), (2, 3, 5), (3, 3, 5), (2, 5, 6), (3, 5, 6),
+        ):
+            passes("tgt", 12 + i, last[i][:], g0, g1)
         tgt_tanh(3)
         tgt_mix(3)
+        tgt_turn(2, 1)
         tgt_turn(3, 2)

from contextlib import ExitStack

import concourse.masks as masks
import concourse.mybir as mybir

F32 = mybir.dt.float32
BF16 = mybir.dt.bfloat16
I32 = mybir.dt.int32
U32 = mybir.dt.uint32
U8 = mybir.dt.uint8
FP8X4 = mybir.dt.float8_e4m3fn_x4
ALU = mybir.AluOpType
ACT = mybir.ActivationFunctionType

P = 128
I_DIM = 1024
H_DIM = 2048
K_DIM = I_DIM + H_DIM
GROUPS = K_DIM // 512
BLOCKS = H_DIM // P
PER_CHUNK = 4
CHUNK = PER_CHUNK * P
CHUNKS = H_DIM // CHUNK
EPS = 1e-6
INV_EPS = 1e6

FLOPS = 2 * P * K_DIM * 2 * H_DIM


def tile_ltccell_w_kernel(
    tc,
    x,
    h,
    time_delta,
    W_mod_words,
    W_mod_scales,
    b_mod,
    W_tgt_words,
    W_tgt_scales,
    b_tgt,
    log_tau,
    bias,
    out,
):
    nc = tc.nc
    with ExitStack() as ctx:
        keep = ctx.enter_context(tc.tile_pool(name="keep", bufs=1))
        work = ctx.enter_context(tc.tile_pool(name="work", bufs=3))
        psz = ctx.enter_context(tc.psum_pool(name="psz", bufs=4))
        pst = ctx.enter_context(tc.psum_pool(name="pst", bufs=4))
        ctx.enter_context(tc.manual_schedule())

        words_mod = keep.tile([P, GROUPS, H_DIM], I32, align_bytes=64)
        words_tgt = keep.tile([P, GROUPS, H_DIM], I32, align_bytes=64)
        planes = keep.tile([P, 4, H_DIM], U8, align_bytes=64)
        c_sb = keep.tile([P, K_DIM], BF16, align_bytes=64)
        grouped = keep.tile([P, GROUPS * 512], BF16, align_bytes=64)
        c_codes = keep.tile([P, GROUPS * P], U32, align_bytes=64)
        c_scales = keep.tile([P, GROUPS * P], U8, align_bytes=64)
        vec_rows = keep.tile([P, P], BF16)
        vec_cols = keep.tile([P, 64], F32)
        dt_all = keep.tile([P, P], F32)
        ident_f = keep.tile([P, P], F32)
        ident_b = keep.tile([P, P], BF16)
        warm = keep.tile([P, 1], F32)
        warm_out = keep.tile([P, 1], F32)
        r_tau = keep.tile([P, BLOCKS], F32)
        shift = keep.tile([P, BLOCKS], F32)
        damp = keep.tile([P, BLOCKS], F32)
        rate = keep.tile([P, BLOCKS], F32)
        q_all = keep.tile([P, H_DIM], F32)
        dh_all = keep.tile([P, H_DIM], F32)

        words = {"mod": words_mod, "tgt": words_tgt}
        src_words = {
            "mod": W_mod_words.rearrange("g p n t -> p g (n t)").bitcast(I32),
            "tgt": W_tgt_words.rearrange("g p n t -> p g (n t)").bitcast(I32),
        }
        h_sb = c_sb[:, I_DIM:K_DIM]
        COL_TAU, COL_MOD, COL_TGT, COL_BIAS, ROW_DT = 0, 16, 32, 48, 64

        def plane_of(w, g):
            if w == "mod":
                return (g // 4, 4 * (g % 4))
            return (2, 4 * g) if g < 4 else (3, 4 * (g - 2))

        nc.vector.memset(warm[:], 0.0)
        for s in (0, 1, 3, 2):
            nc.vector.memset(planes[:, s : s + 1, :].bitcast(I32), 0)
        nc.vector.memset(vec_rows[:].bitcast(I32), 0)
        masks.make_identity(nc, ident_f[:])

        def load_planes(queue, view, slot, k, src, quadrants):
            n_rows = 4 * src.shape[0]
            for q in quadrants:
                queue.dma_start(
                    out=planes[32 * q + k : 32 * q + k + n_rows, slot, :].bitcast(view),
                    in_=src[:, 4 * q : 4 * q + 4, :].bitcast(view),
                )

        def load_words(w, n0, n1, g0, g1):
            nc.sync.dma_start(out=words[w][:, g0:g1, n0:n1], in_=src_words[w][:, g0:g1, n0:n1])

        nc.scalar.activation(out=warm_out[:], in_=warm[:], func=ACT.Exp)
        load_planes(nc.sync, I32, 0, 0, W_mod_scales[0:4], (0, 1, 2, 3))
        load_planes(nc.sync, I32, 1, 0, W_mod_scales[4:6], (0, 1))
        nc.sync.dma_start(out=c_sb[:, 0:I_DIM], in_=x)
        nc.sync.dma_start(out=c_sb[:, I_DIM:K_DIM], in_=h)
        load_planes(nc.sync, I32, 1, 0, W_mod_scales[4:6], (2, 3))
        load_planes(nc.sync, I32, 2, 0, W_tgt_scales[0:4], (0, 1, 2, 3))
        load_planes(nc.gpsimd, F32, 3, 8, W_tgt_scales[4:6], (0, 1, 2, 3))
        masks.make_identity(nc, ident_b[:])
        load_words("mod", 0, 1024, 0, 3)
        for vec, first in ((log_tau, COL_TAU), (b_mod, COL_MOD), (b_tgt, COL_TGT), (bias, COL_BIAS)):
            nc.sync.dma_start(out=vec_rows[first : first + 16, :], in_=vec.rearrange("(c j) -> c j", c=16))
        nc.sync.dma_start(out=vec_rows[ROW_DT : ROW_DT + 1, :], in_=time_delta.rearrange("p o -> o p"))
        for w, n0, n1, cuts in (
            ("mod", 0, 1024, (3, 6)),
            ("mod", 1024, 2048, (0, 3, 6)),
            ("tgt", 0, 512, (0, 3, 6)),
            ("tgt", 512, 1024, (0, 3, 6)),
            ("tgt", 1024, 1536, (0, 3, 6)),
            ("tgt", 1536, 2048, (0, 3)),
            ("tgt", 1536, 1792, (3, 6)),
            ("tgt", 1792, 2048, (3, 5, 6)),
        ):
            for i in range(len(cuts) - 1):
                load_words(w, n0, n1, cuts[i], cuts[i + 1])

        c32 = c_sb[:].bitcast(F32)
        g32 = grouped[:].bitcast(F32).rearrange("p (g t u) -> p g t u", g=GROUPS, t=P, u=2)
        for b in range(3):
            xt = pst.tile([P, 2, 2, P], F32, tag="t", name="xt%d" % b)
            for gi in range(2):
                g = 2 * b + gi
                for u in range(2):
                    nc.tensor.transpose(xt[:, gi, u, :], c32[:, 256 * g + u : 256 * (g + 1) : 2], ident_f[:])
            src = xt[:].rearrange("p g u t -> p g t u")
            if b == 1:
                nc.scalar.copy(out=g32[:, 2 * b : 2 * b + 2], in_=src)
            else:
                nc.vector.tensor_copy(out=g32[:, 2 * b : 2 * b + 2], in_=src)
        nc.vector.quantize_mx(
            out=c_codes[:, 0:256].bitcast(FP8X4), scales=c_scales[:, 0:256], in_=grouped[:, 0:1024]
        )
        nc.vector.quantize_mx(
            out=c_codes[:, 256:768].bitcast(FP8X4),
            scales=c_scales[:, 256:768],
            in_=grouped[:, 1024:3072],
        )

        ps_vec = pst.tile([P, P], BF16, tag="t", name="ps_vec")
        nc.tensor.transpose(ps_vec[:], vec_rows[:], ident_b[:])
        ps_dt = pst.tile([P, P], F32, tag="t", name="ps_dt")
        nc.tensor.matmul(
            ps_dt[:],
            lhsT=ident_b[:, ROW_DT : ROW_DT + 1].to_broadcast([P, P]),
            rhs=vec_rows[:],
            start=True,
            stop=True,
        )
        nc.vector.tensor_copy(out=vec_cols[:], in_=ps_vec[:, 0:64])
        nc.vector.tensor_copy(out=dt_all[:], in_=ps_dt[:])
        nc.scalar.activation(out=r_tau[:], in_=vec_cols[:, COL_TAU : COL_TAU + 16], func=ACT.Exp, scale=-1.0)
        nc.vector.tensor_scalar(
            out=damp[:], in0=r_tau[:], scalar1=EPS, scalar2=1.0, op0=ALU.mult, op1=ALU.add
        )
        nc.vector.scalar_tensor_tensor(
            out=shift[:], in0=r_tau[:], scalar=INV_EPS, in1=r_tau[:], op0=ALU.add, op1=ALU.mult
        )
        nc.vector.reciprocal(out=damp[:], in_=damp[:])
        nc.vector.scalar_tensor_tensor(
            out=rate[:], in0=damp[:], scalar=EPS, in1=damp[:], op0=ALU.mult, op1=ALU.mult
        )

        def passes(w, blk, acc, g0, g1):
            cols = slice(P * blk, P * (blk + 1))
            for g in range(g0, g1):
                slot, k = plane_of(w, g)
                nc.tensor.matmul_mx(
                    out=acc,
                    lhsT=words[w][:, g, cols].bitcast(FP8X4),
                    lhsT_scale=planes[k:P, slot, cols],
                    rhs=c_codes[:, P * g : P * (g + 1)].bitcast(FP8X4),
                    rhs_scale=c_scales[:, P * g : P * (g + 1)],
                    start=(g == 0),
                    stop=(g == GROUPS - 1),
                )

        live = {}

        def mx(w, j):
            z = psz.tile([P, PER_CHUNK, P], F32, tag="z", name="z_%s%d" % (w, j))
            for i in range(PER_CHUNK):
                passes(w, PER_CHUNK * j + i, z[:, i, :], 0, GROUPS)
            live[(w, j)] = [z[:, i, :] for i in range(PER_CHUNK)]

        def block_cols(j, i):
            return slice(CHUNK * j + P * i, CHUNK * j + P * (i + 1))

        def mod_tanh(j):
            g_t = work.tile([P, CHUNK], F32, tag="g", name="g%d" % j)
            live[("g", j)] = g_t
            for i in range(PER_CHUNK):
                c = COL_MOD + PER_CHUNK * j + i
                nc.scalar.activation(
                    out=g_t[:, P * i : P * (i + 1)],
                    in_=live[("mod", j)][i],
                    func=ACT.Abs,
                    bias=vec_cols[:, c : c + 1],
                )
            nc.scalar.activation(out=g_t[:], in_=g_t[:], func=ACT.Tanh)

        def mod_rate(j):
            g_t = live[("g", j)]
            w_t = work.tile([P, CHUNK], F32, tag="w", name="w%d" % j)
            v_t = work.tile([P, CHUNK], F32, tag="v", name="v%d" % j)
            live[("v", j)] = v_t
            nc.vector.scalar_tensor_tensor(
                out=w_t[:], in0=g_t[:], scalar=-INV_EPS, in1=g_t[:], op0=ALU.add, op1=ALU.mult
            )
            for i in range(PER_CHUNK):
                c = PER_CHUNK * j + i
                nc.vector.scalar_tensor_tensor(
                    out=v_t[:, P * i : P * (i + 1)],
                    in0=w_t[:, P * i : P * (i + 1)],
                    scalar=shift[:, c : c + 1],
                    in1=dt_all[:],
                    op0=ALU.subtract,
                    op1=ALU.mult,
                )

        def mod_exp(j):
            v_t = live[("v", j)]
            for i in range(PER_CHUNK):
                c = PER_CHUNK * j + i
                nc.scalar.activation(
                    out=v_t[:, P * i : P * (i + 1)],
                    in_=v_t[:, P * i : P * (i + 1)],
                    func=ACT.Exp,
                    scale=rate[:, c : c + 1],
                )

        def mod_rest(j):
            nc.vector.tensor_scalar(
                out=q_all[:, CHUNK * j : CHUNK * (j + 1)],
                in0=live[("v", j)][:],
                scalar1=-1.0,
                scalar2=1.0,
                op0=ALU.mult,
                op1=ALU.add,
            )

        def mod_turn(j):
            v_t = live[("v", j)]
            ps = pst.tile([P, CHUNK], F32, tag="t", name="ps_d%d" % j)
            for i in range(PER_CHUNK):
                nc.tensor.transpose(ps[:, P * i : P * (i + 1)], v_t[:, P * i : P * (i + 1)], ident_f[:])
            cols = slice(CHUNK * j, CHUNK * (j + 1))
            nc.vector.tensor_tensor(out=dh_all[:, cols], in0=ps[:], in1=h_sb[:, cols], op=ALU.mult)

        def tgt_tanh(j):
            a_t = work.tile([P, CHUNK], F32, tag="a", name="a%d" % j)
            live[("a", j)] = a_t
            for i in range(PER_CHUNK):
                c = COL_TGT + PER_CHUNK * j + i
                nc.scalar.activation(
                    out=a_t[:, P * i : P * (i + 1)],
                    in_=live[("tgt", j)][i],
                    func=ACT.Tanh,
                    bias=vec_cols[:, c : c + 1],
                )

        def tgt_mix(j, blocks=range(PER_CHUNK)):
            a_t = live[("a", j)]
            for i in blocks:
                c = COL_BIAS + PER_CHUNK * j + i
                nc.vector.scalar_tensor_tensor(
                    out=a_t[:, P * i : P * (i + 1)],
                    in0=a_t[:, P * i : P * (i + 1)],
                    scalar=vec_cols[:, c : c + 1],
                    in1=q_all[:, block_cols(j, i)],
                    op0=ALU.add,
                    op1=ALU.mult,
                )

        def tgt_turn(j, pieces):
            a_t = live[("a", j)]
            o_t = work.tile([P, CHUNK], F32, tag="o", name="o%d" % j)
            n = PER_CHUNK // pieces
            width = n * P
            turned = []
            for s in range(pieces):
                ps = pst.tile([P, width], F32, tag="t", name="ps_u%d_%d" % (j, s))
                turned.append(ps)
                for i in range(n):
                    b = n * s + i
                    nc.tensor.transpose(ps[:, P * i : P * (i + 1)], a_t[:, P * b : P * (b + 1)], ident_f[:])
            for s in range(pieces):
                cols = slice(CHUNK * j + width * s, CHUNK * j + width * (s + 1))
                o_cols = slice(width * s, width * (s + 1))
                nc.vector.tensor_tensor(
                    out=o_t[:, o_cols], in0=turned[s][:], in1=dh_all[:, cols], op=ALU.add
                )
                nc.sync.dma_start(out=out[:, cols], in_=o_t[:, o_cols])

        mx("mod", 0)
        mod_tanh(0)
        mod_rate(0)
        mx("mod", 1)
        mod_tanh(1)
        mod_exp(0)
        mod_rate(1)
        mod_rest(0)
        mod_exp(1)
        mod_rest(1)
        mx("mod", 2)
        mod_tanh(2)
        mod_turn(0)
        mod_rate(2)
        mx("mod", 3)
        mod_tanh(3)
        mod_exp(2)
        mod_turn(1)
        mod_rate(3)
        mod_rest(2)
        mx("tgt", 0)
        mod_exp(3)
        tgt_tanh(0)
        mod_turn(2)
        mod_rest(3)
        tgt_mix(0)
        mx("tgt", 1)
        tgt_tanh(1)
        mod_turn(3)
        tgt_mix(1)
        tgt_turn(0, 1)
        mx("tgt", 2)
        tgt_tanh(2)
        tgt_mix(2, (0, 1))
        tgt_turn(1, 1)
        tgt_mix(2, (2, 3))
        last = [psz.tile([P, P], F32, tag="z", name="z_last%d" % i) for i in range(PER_CHUNK)]
        live[("tgt", 3)] = [t[:] for t in last]
        for i, g0, g1 in (
            (0, 0, 3), (1, 0, 3), (2, 0, 3), (3, 0, 3),
            (0, 3, 6), (1, 3, 6), (2, 3, 5), (3, 3, 5), (2, 5, 6), (3, 5, 6),
        ):
            passes("tgt", 12 + i, last[i][:], g0, g1)
        tgt_tanh(3)
        tgt_mix(3)
        tgt_turn(2, 1)
        tgt_turn(3, 2)
